import numpy as np
import ml_dtypes


def mxq(x, axis, fmt="e4m3"):
    dtype, down = {"e4m3": (ml_dtypes.float8_e4m3fn, 7), "e5m2": (ml_dtypes.float8_e5m2, 14)}[fmt]
    v = np.moveaxis(np.asarray(x, np.float32).astype(ml_dtypes.bfloat16).astype(np.float64), axis, -1)
    blocks = v.reshape(v.shape[:-1] + (-1, 32))
    amax = np.abs(blocks).max(-1, keepdims=True)
    byte = np.maximum(np.where(amax > 0, np.frexp(amax)[1] - 1 + 127, 0) - down, 1)
    scale = np.exp2(byte - 127.0)
    codes = (blocks / scale).astype(np.float32).astype(dtype).astype(np.float64)
    return np.moveaxis((codes * scale).reshape(v.shape), -1, axis)


WIDE = False


def mx_kscale(k):
    if not WIDE:
        return np.ones(k)
    levels = np.array([10, -10, 5, -5, 0])
    a = np.random.permutation(np.resize(levels, k // 512 * 4)).reshape(k // 512, 4)
    idx = np.arange(k)
    return np.exp2(a[idx // 512, idx % 128 // 32])


BF16 = ml_dtypes.bfloat16


def bf(x):
    return np.asarray(x, np.float32).astype(BF16)


def f64(x):
    return np.asarray(x).astype(np.float64)


B, T, D, M, C = 4, 128, 2048, 512, 8192


def sigmoid(v):
    return 1.0 / (1.0 + np.exp(-v))


def setup_inputs():
    t = mx_kscale(M)
    go_w = np.concatenate([np.random.standard_normal((M, D)) / np.sqrt(D),
                           np.random.standard_normal((M, M)) * 2.0 / np.sqrt(M) / t], axis=1)
    return {"h": bf(np.random.standard_normal((B, T, D))),
            "gated_mem": bf(np.random.standard_normal((B, T, M)) * 0.4 * t),
            "go_w": bf(go_w),
            "go_b": bf(np.random.standard_normal(M) * 0.5),
            "out_w": bf(np.random.standard_normal((D, M)) * 5.0 / np.sqrt(M) / t),
            "out_b": bf(np.random.standard_normal(D) * 0.5)}


def reference(h, gated_mem, go_w, go_b, out_w, out_b):
    h = f64(h)
    g = f64(gated_mem)
    gate_in = np.concatenate([h, g], axis=-1)
    gate_w = sigmoid((mxq(gate_in, 2, "e4m3") @ mxq(f64(go_w), 1, "e4m3").T) + f64(go_b))
    return h + (mxq(gate_w * g, 2, "e4m3") @ mxq(f64(out_w), 1, "e4m3").T) + f64(out_b)

@@ -1,0 +1,283 @@
+from contextlib import ExitStack
+
+import concourse.mybir as mybir
+from concourse.masks import make_identity
+
+F32 = mybir.dt.float32
+BF16 = mybir.dt.bfloat16
+U32 = mybir.dt.uint32
+U8 = mybir.dt.uint8
+FP8X4 = mybir.dt.float8_e4m3fn_x4
+ADD = mybir.AluOpType.add
+MULT = mybir.AluOpType.mult
+SIGMOID = mybir.ActivationFunctionType.Sigmoid
+
+P = 128
+TOK = 512
+D = 2048
+M = 512
+K1 = D + M
+PASSES1 = K1 // 512
+
+FLOPS = 2 * TOK * K1 * M + 2 * TOK * M * D
+
+MANUAL = True
+HB_ON_GPSIMD = ((2, 0), (2, 1), (2, 2), (2, 3), (3, 0), (3, 1), (3, 2), (3, 3))
+EXIT_ON_VECTOR = ()
+N_BANKS = 6
+N_GROUPED = 4
+
+
+def tile_aurelianmemorycore_pb_kernel(tc, h, gated_mem, go_w, go_b, out_w, out_b, out):
+    nc = tc.nc
+    h_v = h.flatten_outer_dims().rearrange("(p t) d -> p t d", t=4)
+    g_v = gated_mem.flatten_outer_dims().rearrange("(p t) m -> p t m", t=4)
+    gw_v = go_w.rearrange("(u p e) k -> p u e k", u=2, e=2)
+    ow_v = out_w.rearrange("(v p e) k -> p v e k", p=P, e=2)
+    out_v = out.flatten_outer_dims().rearrange("(p t) d -> p t d", t=4)
+
+    with ExitStack() as ctx:
+        keep = ctx.enter_context(tc.tile_pool(name="keep", bufs=1))
+        grp = ctx.enter_context(tc.tile_pool(name="grp", bufs=N_GROUPED))
+        prod = ctx.enter_context(tc.tile_pool(name="prod", bufs=2))
+        banks = ctx.enter_context(tc.psum_pool(name="banks", bufs=N_BANKS))
+        ps1 = ctx.enter_context(tc.psum_pool(name="ps1", bufs=2))
+        if MANUAL:
+            ctx.enter_context(tc.manual_schedule())
+
+        zrow = keep.tile([P, D], BF16)
+        zb = keep.tile([P, 2 * P], BF16)
+        ones = keep.tile([P, P], BF16)
+        warm = keep.tile([P, 2], F32)
+        ident = keep.tile([P, P], F32)
+        nc.vector.memset(zrow[:], 0.0)
+        nc.vector.memset(zb[:], 0.0)
+        nc.vector.memset(ones[:], 1.0)
+        nc.vector.memset(warm[:], 0.0)
+        make_identity(nc, ident[:])
+        nc.scalar.activation(out=warm[:, 1:2], in_=warm[:, 0:1], func=SIGMOID)
+
+        h_a = [keep.tile([P, 2, 1024], BF16, name="h_a%d" % i) for i in range(2)]
+        g_a = keep.tile([P, 2, M], BF16)
+        gw_cols = ((0, 1024), (1024, K1))
+        gw_sb = [[keep.tile([P, 2, hi - lo], BF16, name="gw_sb%d_%d" % (um, lo)) for (lo, hi) in gw_cols] for um in range(2)]
+        ow_sb = [keep.tile([P, 2, 2, M], BF16, name="ow_sb%d" % q) for q in range(4)]
+        g_b = keep.tile([P, 2, M], BF16)
+        h_b = [keep.tile([P, D], BF16, name="h_b%d" % i) for i in range(2)]
+        nc.sync.dma_start(out=h_a[0][:], in_=h_v[:, 0:2, 0:1024])
+        nc.sync.dma_start(out=zrow[0:1, :], in_=out_b.rearrange("(o d) -> o d", o=1))
+        nc.sync.dma_start(out=zb[0:2, :], in_=go_b.rearrange("(u x) -> u x", u=2))
+        nc.sync.dma_start(out=h_a[1][:], in_=h_v[:, 0:2, 1024:2048])
+        nc.sync.dma_start(out=g_a[:], in_=g_v[:, 0:2, :])
+        for um in range(2):
+            for i, (lo, hi) in enumerate(gw_cols):
+                nc.sync.dma_start(out=gw_sb[um][i][:], in_=gw_v[:, um, :, lo:hi])
+        for q in range(4):
+            nc.sync.dma_start(out=ow_sb[q][:], in_=ow_v[:, 2 * q : 2 * q + 2, :, :])
+        nc.sync.dma_start(out=g_b[:], in_=g_v[:, 2:4, :])
+        for i in range(2):
+            nc.sync.dma_start(out=h_b[i][:], in_=h_v[:, 2 + i, :])
+
+        def h_block(tt, c):
+            if tt < 2:
+                return h_a[c // 2][:, tt, 512 * (c % 2) : 512 * (c % 2) + 512]
+            return h_b[tt - 2][:, 512 * c : 512 * c + 512]
+
+        def gate_in_block(tt, c):
+            if c < 4:
+                return h_block(tt, c)
+            return g_a[:, tt, :] if tt < 2 else g_b[:, tt - 2, :]
+
+        def gw_block(um, e, c):
+            if c < 2:
+                return gw_sb[um][0][:, e, 512 * c : 512 * c + 512]
+            return gw_sb[um][1][:, e, 512 * (c - 2) : 512 * (c - 2) + 512]
+
+        gia_c = keep.tile([P, PASSES1 * 256], U32, align_bytes=64)
+        gia_s = keep.tile([P, PASSES1 * 256], U8, align_bytes=64)
+        gib_c = [keep.tile([P, PASSES1 * P], U32, align_bytes=64, name="gib_c%d" % i) for i in range(2)]
+        gib_s = [keep.tile([P, PASSES1 * P], U8, align_bytes=64, name="gib_s%d" % i) for i in range(2)]
+        gw_c = keep.tile([P, PASSES1 * M], U32, align_bytes=64)
+        gw_s = keep.tile([P, PASSES1 * M], U8, align_bytes=64)
+        ow_c = keep.tile([P, D], U32, align_bytes=64)
+        ow_s = keep.tile([P, D], U8, align_bytes=64)
+        p_c = keep.tile([P, TOK], U32, align_bytes=64)
+        p_s = keep.tile([P, TOK], U8, align_bytes=64)
+        gq = keep.tile([P, 4 * M], BF16, align_bytes=64)
+        sig_a = keep.tile([P, 4, 256], F32)
+        sig_b = [keep.tile([P, 4, P], F32, name="sig_b%d" % i) for i in range(2)]
+        hb = [keep.tile([P, D], F32, name="hb%d" % tt) for tt in range(4)]
+        bbc = keep.tile([P, D], F32)
+        gob = keep.tile([P, 4], F32)
+
+        for j in range(4):
+            bb = banks.tile([P, 512], F32, tag="bank")
+            nc.tensor.matmul(out=bb[:], lhsT=ones[:], rhs=zrow[:, 512 * j : 512 * j + 512], start=True, stop=True)
+            nc.scalar.copy(out=bbc[:, 512 * j : 512 * j + 512], in_=bb[:])
+        tb = banks.tile([P, P], F32, tag="bank")
+        nc.tensor.transpose(tb[:], zb[:].bitcast(F32), ident[:])
+        nc.vector.tensor_copy(out=gob[:], in_=tb[:, 0:2].bitcast(BF16))
+
+        def residual(tt, j):
+            eng = nc.gpsimd if (tt, j) in HB_ON_GPSIMD else nc.vector
+            cols = slice(512 * j, 512 * j + 512)
+            eng.tensor_tensor(out=hb[tt][:, cols], in0=h_block(tt, j), in1=bbc[:, cols], op=ADD)
+
+        for tt in range(4):
+            for j in range(4):
+                if (tt, j) in HB_ON_GPSIMD:
+                    residual(tt, j)
+        hb_vector = [(tt, j) for tt in range(4) for j in range(4) if (tt, j) not in HB_ON_GPSIMD]
+
+        pending = []
+        count = [0]
+
+        def flush():
+            while pending:
+                codes, scales, grouped = pending.pop(0)
+                nc.vector.quantize_mx(out=codes.bitcast(FP8X4), scales=scales, in_=grouped)
+
+        def run(blocks, codes, scales, mix=False, grouped=None):
+            a = len(blocks)
+            xt = banks.tile([P, a, 2, P], F32, tag="bank")
+            for i, src in enumerate(blocks):
+                words = src.bitcast(F32)
+                for u in range(2):
+                    nc.tensor.transpose(xt[:, i, u, :], words[:, P * u : P * u + P], ident[:])
+            if grouped is None:
+                gt = grp.tile([P, 1024], BF16, tag="grp", align_bytes=64)
+                grouped = gt[:, 0 : 512 * a]
+            gf = grouped.bitcast(F32)
+            if mix:
+                dst = gf.rearrange("p (r a u) -> p r a u", a=a, u=2)
+                src_v = xt[:].rearrange("p a u r -> p r a u")
+            else:
+                dst = gf.rearrange("p (a r u) -> p a r u", a=a, u=2)
+                src_v = xt[:].rearrange("p a u r -> p a r u")
+            if count[0] in EXIT_ON_VECTOR:
+                nc.vector.tensor_copy(out=dst, in_=src_v)
+            else:
+                nc.scalar.copy(out=dst, in_=src_v)
+            count[0] += 1
+            flush()
+            pending.append((codes, scales, grouped))
+
+        def run_gia(c):
+            cols = slice(256 * c, 256 * c + 256)
+            run([gate_in_block(0, c), gate_in_block(1, c)], gia_c[:, cols], gia_s[:, cols],
+                grouped=gq[:, 0:1024] if c == 4 else None)
+
+        def run_gw(um, c):
+            cols = slice(512 * c + 256 * um, 512 * c + 256 * um + 256)
+            run([gw_block(um, 0, c), gw_block(um, 1, c)], gw_c[:, cols], gw_s[:, cols])
+
+        def run_ow(v):
+            cols = slice(256 * v, 256 * v + 256)
+            run([ow_sb[v // 2][:, v % 2, 0, :], ow_sb[v // 2][:, v % 2, 1, :]], ow_c[:, cols], ow_s[:, cols], mix=True)
+
+        def run_gib(tt, s):
+            cs = ((0, 1), (2, 3), (4,))[s]
+            cols = slice(P * cs[0], P * cs[0] + P * len(cs))
+            run([gate_in_block(tt, c) for c in cs], gib_c[tt - 2][:, cols], gib_s[tt - 2][:, cols],
+                grouped=gq[:, 512 * tt : 512 * tt + 512] if s == 2 else None)
+
+        def gate(gi_c, gi_s, n, um, sig):
+            acc = ps1.tile([P, 2, n], F32, tag="acc1")
+            for e in range(2):
+                t = 2 * um + e
+                for c in range(PASSES1):
+                    w = slice(512 * c + P * t, 512 * c + P * t + P)
+                    x = slice(n * c, n * c + n)
+                    nc.tensor.matmul_mx(out=acc[:, e, :], lhsT=gw_c[:, w].bitcast(FP8X4), lhsT_scale=gw_s[:, w],
+                                        rhs=gi_c[:, x].bitcast(FP8X4), rhs_scale=gi_s[:, x],
+                                        start=(c == 0), stop=(c == PASSES1 - 1))
+            for e in range(2):
+                t = 2 * um + e
+                nc.scalar.activation(out=sig[:, t, :], in_=acc[:, e, :], func=SIGMOID, bias=gob[:, t : t + 1], scale=1.0)
+
+        held = {}
+
+        def product(tt):
+            sig = sig_a[:, :, P * tt : P * tt + P] if tt < 2 else sig_b[tt - 2][:]
+            pg = prod.tile([P, 512], BF16, tag="pg", align_bytes=64)
+            nc.vector.tensor_tensor(out=pg[:].rearrange("p (r t) -> p r t", t=4), in0=sig.rearrange("p t r -> p r t"),
+                                    in1=gq[:, 512 * tt : 512 * tt + 512].rearrange("p (r t) -> p r t", t=4), op=MULT)
+            held[tt] = pg
+
+        def quantise_product(tt):
+            cols = slice(P * tt, P * tt + P)
+            nc.vector.quantize_mx(out=p_c[:, cols].bitcast(FP8X4), scales=p_s[:, cols], in_=held[tt][:])
+
+        def fuse(tt, js):
+            accs = []
+            for j in js:
+                acc2 = banks.tile([P, 512], F32, tag="bank")
+                t_cols = slice(P * tt, P * tt + P)
+                d_cols = slice(512 * j, 512 * j + 512)
+                nc.tensor.matmul_mx(out=acc2[:], lhsT=p_c[:, t_cols].bitcast(FP8X4), lhsT_scale=p_s[:, t_cols],
+                                    rhs=ow_c[:, d_cols].bitcast(FP8X4), rhs_scale=ow_s[:, d_cols], start=True, stop=True)
+                accs.append(acc2)
+            for j, acc2 in zip(js, accs):
+                d_cols = slice(512 * j, 512 * j + 512)
+                nc.vector.tensor_tensor(out=hb[tt][:, d_cols], in0=acc2[:], in1=hb[tt][:, d_cols], op=ADD)
+
+        def store(tt, dh):
+            cols = slice(1024 * dh, 1024 * dh + 1024)
+            nc.sync.dma_start(out=out_v[:, tt, cols], in_=hb[tt][:, cols])
+
+        def some_residual(n):
+            for i in range(n):
+                if hb_vector:
+                    tt, j = hb_vector.pop(0)
+                    residual(tt, j)
+
+        for c in range(PASSES1):
+            run_gia(c)
+            some_residual(c % 2)
+        for c in range(PASSES1):
+            run_gw(0, c)
+            some_residual(c % 2)
+        run_gw(1, 0)
+        run_gw(1, 1)
+        some_residual(1)
+        gate(gia_c, gia_s, 256, 0, sig_a)
+        for c in range(2, PASSES1):
+            run_gw(1, c)
+            some_residual(c % 2)
+        run_ow(0)
+        run_ow(1)
+        flush()
+        some_residual(16)
+        gate(gia_c, gia_s, 256, 1, sig_a)
+        product(0)
+        product(1)
+        quantise_product(0)
+        quantise_product(1)
+        for v in range(2, 8):
+            run_ow(v)
+        flush()
+        late = [(tt, s) for tt in (2, 3) for s in range(3)]
+        for tt in (0, 1):
+            for dh in (0, 1):
+                fuse(tt, (2 * dh, 2 * dh + 1))
+                store(tt, dh)
+                b_tt, b_s = late.pop(0)
+                run_gib(b_tt, b_s)
+        for b_tt, b_s in late:
+            run_gib(b_tt, b_s)
+        flush()
+        for tt in (2, 3):
+            for um in range(2):
+                gate(gib_c[tt - 2], gib_s[tt - 2], P, um, sig_b[tt - 2])
+        product(2)
+        quantise_product(2)
+        fuse(2, (0,))
+        product(3)
+        quantise_product(3)
+        fuse(2, (1,))
+        store(2, 0)
+        fuse(2, (2, 3))
+        store(2, 1)
+        for dh in (0, 1):
+            fuse(3, (2 * dh, 2 * dh + 1))
+            store(3, dh)

@@ -24,8 +24,8 @@ FLOPS = 2 * TOK * K1 * M + 2 * TOK * M * D
 MANUAL = True
 HB_ON_GPSIMD = ((2, 0), (2, 1), (2, 2), (2, 3), (3, 0), (3, 1), (3, 2), (3, 3))
 EXIT_ON_VECTOR = ()
-N_BANKS = 6
-N_GROUPED = 4
+N_BANKS = 4
+N_GROUPED = 6
 
 
 def tile_aurelianmemorycore_pb_kernel(tc, h, gated_mem, go_w, go_b, out_w, out_b, out):
@@ -41,7 +41,7 @@ def tile_aurelianmemorycore_pb_kernel(tc, h, gated_mem, go_w, go_b, out_w, out_b
         grp = ctx.enter_context(tc.tile_pool(name="grp", bufs=N_GROUPED))
         prod = ctx.enter_context(tc.tile_pool(name="prod", bufs=2))
         banks = ctx.enter_context(tc.psum_pool(name="banks", bufs=N_BANKS))
-        ps1 = ctx.enter_context(tc.psum_pool(name="ps1", bufs=2))
+        ps1 = ctx.enter_context(tc.psum_pool(name="ps1", bufs=4))
         if MANUAL:
             ctx.enter_context(tc.manual_schedule())
 
@@ -59,7 +59,7 @@ def tile_aurelianmemorycore_pb_kernel(tc, h, gated_mem, go_w, go_b, out_w, out_b
 
         h_a = [keep.tile([P, 2, 1024], BF16, name="h_a%d" % i) for i in range(2)]
         g_a = keep.tile([P, 2, M], BF16)
-        gw_cols = ((0, 1024), (1024, K1))
+        gw_cols = ((0, 1024), (1024, 2048), (2048, K1))
         gw_sb = [[keep.tile([P, 2, hi - lo], BF16, name="gw_sb%d_%d" % (um, lo)) for (lo, hi) in gw_cols] for um in range(2)]
         ow_sb = [keep.tile([P, 2, 2, M], BF16, name="ow_sb%d" % q) for q in range(4)]
         g_b = keep.tile([P, 2, M], BF16)
@@ -69,8 +69,8 @@ def tile_aurelianmemorycore_pb_kernel(tc, h, gated_mem, go_w, go_b, out_w, out_b
         nc.sync.dma_start(out=zb[0:2, :], in_=go_b.rearrange("(u x) -> u x", u=2))
         nc.sync.dma_start(out=h_a[1][:], in_=h_v[:, 0:2, 1024:2048])
         nc.sync.dma_start(out=g_a[:], in_=g_v[:, 0:2, :])
-        for um in range(2):
-            for i, (lo, hi) in enumerate(gw_cols):
+        for i, (lo, hi) in enumerate(gw_cols):
+            for um in range(2):
                 nc.sync.dma_start(out=gw_sb[um][i][:], in_=gw_v[:, um, :, lo:hi])
         for q in range(4):
             nc.sync.dma_start(out=ow_sb[q][:], in_=ow_v[:, 2 * q : 2 * q + 2, :, :])
@@ -89,9 +89,7 @@ def tile_aurelianmemorycore_pb_kernel(tc, h, gated_mem, go_w, go_b, out_w, out_b
             return g_a[:, tt, :] if tt < 2 else g_b[:, tt - 2, :]
 
         def gw_block(um, e, c):
-            if c < 2:
-                return gw_sb[um][0][:, e, 512 * c : 512 * c + 512]
-            return gw_sb[um][1][:, e, 512 * (c - 2) : 512 * (c - 2) + 512]
+            return gw_sb[um][c // 2][:, e, 512 * (c % 2) : 512 * (c % 2) + 512]
 
         gia_c = keep.tile([P, PASSES1 * 256], U32, align_bytes=64)
         gia_s = keep.tile([P, PASSES1 * 256], U8, align_bytes=64)
@@ -110,23 +108,26 @@ def tile_aurelianmemorycore_pb_kernel(tc, h, gated_mem, go_w, go_b, out_w, out_b
         bbc = keep.tile([P, D], F32)
         gob = keep.tile([P, 4], F32)
 
-        for j in range(4):
-            bb = banks.tile([P, 512], F32, tag="bank")
-            nc.tensor.matmul(out=bb[:], lhsT=ones[:], rhs=zrow[:, 512 * j : 512 * j + 512], start=True, stop=True)
-            nc.scalar.copy(out=bbc[:, 512 * j : 512 * j + 512], in_=bb[:])
-        tb = banks.tile([P, P], F32, tag="bank")
-        nc.tensor.transpose(tb[:], zb[:].bitcast(F32), ident[:])
-        nc.vector.tensor_copy(out=gob[:], in_=tb[:, 0:2].bitcast(BF16))
+        def biases():
+            for j in range(4):
+                bb = banks.tile([P, 512], F32, tag="bank")
+                nc.tensor.matmul(out=bb[:], lhsT=ones[:], rhs=zrow[:, 512 * j : 512 * j + 512], start=True, stop=True)
+                nc.vector.tensor_copy(out=bbc[:, 512 * j : 512 * j + 512], in_=bb[:])
+            tb = banks.tile([P, P], F32, tag="bank")
+            nc.tensor.transpose(tb[:], zb[:].bitcast(F32), ident[:])
+            nc.vector.tensor_copy(out=gob[:], in_=tb[:, 0:2].bitcast(BF16))
 
         def residual(tt, j):
             eng = nc.gpsimd if (tt, j) in HB_ON_GPSIMD else nc.vector
             cols = slice(512 * j, 512 * j + 512)
             eng.tensor_tensor(out=hb[tt][:, cols], in0=h_block(tt, j), in1=bbc[:, cols], op=ADD)
 
-        for tt in range(4):
-            for j in range(4):
-                if (tt, j) in HB_ON_GPSIMD:
-                    residual(tt, j)
+        def residual_on_gpsimd():
+            for tt in range(4):
+                for j in range(4):
+                    if (tt, j) in HB_ON_GPSIMD:
+                        residual(tt, j)
+
         hb_vector = [(tt, j) for tt in range(4) for j in range(4) if (tt, j) not in HB_ON_GPSIMD]
 
         pending = []
@@ -195,6 +196,23 @@ def tile_aurelianmemorycore_pb_kernel(tc, h, gated_mem, go_w, go_b, out_w, out_b
                 t = 2 * um + e
                 nc.scalar.activation(out=sig[:, t, :], in_=acc[:, e, :], func=SIGMOID, bias=gob[:, t : t + 1], scale=1.0)
 
+        acc_a = []
+
+        def gate_a_passes(c):
+            if c == 0:
+                for t in range(4):
+                    acc_a.append(ps1.tile([P, 256], F32, tag="acc1", name="acc_a%d" % t))
+            x = slice(256 * c, 256 * c + 256)
+            for t in range(4):
+                w = slice(512 * c + P * t, 512 * c + P * t + P)
+                nc.tensor.matmul_mx(out=acc_a[t][:], lhsT=gw_c[:, w].bitcast(FP8X4), lhsT_scale=gw_s[:, w],
+                                    rhs=gia_c[:, x].bitcast(FP8X4), rhs_scale=gia_s[:, x],
+                                    start=(c == 0), stop=(c == PASSES1 - 1))
+
+        def gate_a_sigmoid():
+            for t in range(4):
+                nc.scalar.activation(out=sig_a[:, t, :], in_=acc_a[t][:], func=SIGMOID, bias=gob[:, t : t + 1], scale=1.0)
+
         held = {}
 
         def product(tt):
@@ -231,38 +249,44 @@ def tile_aurelianmemorycore_pb_kernel(tc, h, gated_mem, go_w, go_b, out_w, out_b
                     tt, j = hb_vector.pop(0)
                     residual(tt, j)
 
-        for c in range(PASSES1):
+        run_gia(0)
+        run_gia(1)
+        flush()
+        biases()
+        residual_on_gpsimd()
+        for c in range(2, PASSES1):
             run_gia(c)
-            some_residual(c % 2)
+            some_residual(1)
         for c in range(PASSES1):
             run_gw(0, c)
-            some_residual(c % 2)
-        run_gw(1, 0)
-        run_gw(1, 1)
-        some_residual(1)
-        gate(gia_c, gia_s, 256, 0, sig_a)
-        for c in range(2, PASSES1):
             run_gw(1, c)
-            some_residual(c % 2)
+            some_residual(1)
+            if c > 0:
+                gate_a_passes(c - 1)
         run_ow(0)
-        run_ow(1)
+        gate_a_passes(PASSES1 - 1)
+        gate_a_sigmoid()
         flush()
         some_residual(16)
-        gate(gia_c, gia_s, 256, 1, sig_a)
         product(0)
         product(1)
         quantise_product(0)
         quantise_product(1)
-        for v in range(2, 8):
+        for v in range(1, 5):
             run_ow(v)
-        flush()
+        fuse(0, (0, 1))
+        store(0, 0)
+        run_ow(5)
+        fuse(1, (0, 1))
+        store(1, 0)
+        run_ow(6)
+        run_ow(7)
         late = [(tt, s) for tt in (2, 3) for s in range(3)]
         for tt in (0, 1):
-            for dh in (0, 1):
-                fuse(tt, (2 * dh, 2 * dh + 1))
-                store(tt, dh)
-                b_tt, b_s = late.pop(0)
-                run_gib(b_tt, b_s)
+            b_tt, b_s = late.pop(0)
+            run_gib(b_tt, b_s)
+            fuse(tt, (2, 3))
+            store(tt, 1)
         for b_tt, b_s in late:
             run_gib(b_tt, b_s)
         flush()

@@ -21,11 +21,49 @@ PASSES1 = K1 // 512
 
 FLOPS = 2 * TOK * K1 * M + 2 * TOK * M * D
 
+CURRENT = [None]
 MANUAL = True
+GROUPS = ((0, 1), (2,), (3,))
 HB_ON_GPSIMD = ((2, 0), (2, 1), (2, 2), (2, 3), (3, 0), (3, 1), (3, 2), (3, 3))
 EXIT_ON_VECTOR = ()
-N_BANKS = 4
+BIAS_COPY = "v"
+N_BANKS = 6
+N_ACC1 = 2
 N_GROUPED = 6
+LOADS = ("h0a", "ob", "gb", "h0b", "g0", "w00", "w01", "w10", "w11", "w20", "w21", "o0", "o1", "o2", "o3", "g1", "h1", "g2", "h2")
+ORDER = (
+    ("T", "i0_0"), ("GT", 0), ("BM", 0), ("X", "i0_0"), ("GC", 0), ("BM", 1),
+    ("BC", 0), ("BM", 3), ("BM", 2), ("BC", 1), ("T", "i0_2"), ("BC", 3),
+    ("T", "i0_4"), ("X", "i0_2"), ("BC", 2), ("T", "w0_0"), ("X", "i0_4"), ("T", "i0_8"),
+    ("Q", "i0_2"), ("T", "w0_1"), ("X", "w0_0"), ("Q", "i0_0"), ("T", "i0_6"), ("Q", "i0_4"),
+    ("T", "w1_0"), ("X", "i0_8"), ("HB", 0, 0), ("T", "w1_1"), ("X", "i0_6"), ("Q", "w0_0"),
+    ("Q", "i0_8"), ("T", "w0_3"), ("X", "w1_0"), ("HB", 0, 1), ("T", "w0_2"), ("X", "w1_1"),
+    ("Q", "i0_6"), ("T", "w1_3"), ("Q", "w1_0"), ("X", "w0_1"), ("HB", 0, 3), ("T", "w1_2"),
+    ("X", "w0_3"), ("T", "w0_4"), ("Q", "w0_1"), ("Q", "w1_1"), ("T", "w1_4"), ("X", "w0_2"),
+    ("Q", "w0_3"), ("HB", 0, 2), ("X", "w1_3"), ("T", "o0"), ("X", "w1_2"), ("Q", "w0_2"),
+    ("Q", "w1_3"), ("X", "w0_4"), ("HB", 1, 3), ("T", "o1"), ("T", "o2"), ("X", "w1_4"),
+    ("Q", "w1_2"), ("T", "o3"), ("Q", "w0_4"), ("X", "o2"), ("HB", 1, 1), ("G", 0, 0),
+    ("X", "o3"), ("Q", "w1_4"), ("G", 0, 2), ("Q", "o2"), ("X", "o0"), ("HB", 1, 0),
+    ("G", 0, 1), ("X", "o1"), ("Q", "o3"), ("Q", "o0"), ("G", 0, 3), ("HB", 1, 2),
+    ("S", 0, 0), ("S", 0, 1), ("Q", "o1"), ("T", "o4"), ("HB", 2, 0), ("S", 0, 3),
+    ("T", "i1_0"), ("S", 0, 2), ("T", "i1_2"), ("X", "o4"), ("T", "o5"), ("PR", 0),
+    ("HB", 2, 1), ("T", "o6"), ("X", "i1_0"), ("Q", "o4"), ("T", "i1_4"), ("T", "o7"),
+    ("QP", 0), ("X", "i1_2"), ("PR", 1), ("HB", 2, 3), ("X", "o5"), ("F", 0, 0),
+    ("Q", "i1_0"), ("F", 0, 1), ("Q", "i1_2"), ("X", "i1_4"), ("A", 0, 0), ("X", "o6"),
+    ("T", "i2_0"), ("HB", 3, 2), ("Q", "i1_4"), ("G", 1, 2), ("X", "o7"), ("Q", "o5"),
+    ("Q", "o6"), ("X", "i2_0"), ("G", 1, 0), ("A", 0, 1), ("HB", 3, 3), ("G", 1, 1),
+    ("Q", "o7"), ("G", 1, 3), ("ST", 0, 0), ("S", 1, 0), ("Q", "i2_0"), ("F", 0, 2),
+    ("S", 1, 1), ("QP", 1), ("HB", 3, 1), ("S", 1, 2), ("T", "i2_2"), ("S", 1, 3),
+    ("A", 0, 2), ("T", "i2_4"), ("X", "i2_2"), ("F", 0, 3), ("PR", 2), ("F", 1, 2),
+    ("HB", 3, 0), ("X", "i2_4"), ("F", 1, 3), ("A", 0, 3), ("F", 1, 0), ("F", 1, 1),
+    ("Q", "i2_2"), ("HB", 2, 2), ("ST", 0, 1), ("Q", "i2_4"), ("G", 2, 2), ("QP", 2),
+    ("A", 1, 2), ("G", 2, 0), ("A", 1, 3), ("G", 2, 1), ("G", 2, 3), ("A", 1, 1),
+    ("S", 2, 1), ("F", 2, 1), ("S", 2, 0), ("S", 2, 3), ("F", 2, 0), ("A", 1, 0),
+    ("S", 2, 2), ("F", 2, 3), ("PR", 3), ("ST", 1, 0), ("F", 2, 2), ("ST", 1, 1),
+    ("A", 2, 0), ("A", 2, 1), ("QP", 3), ("A", 2, 2), ("ST", 2, 0), ("F", 3, 0),
+    ("A", 2, 3), ("F", 3, 2), ("F", 3, 1), ("A", 3, 0), ("F", 3, 3), ("ST", 2, 1),
+    ("A", 3, 1), ("A", 3, 2), ("ST", 3, 0), ("A", 3, 3), ("ST", 3, 1),
+)
 
 
 def tile_aurelianmemorycore_pb_kernel(tc, h, gated_mem, go_w, go_b, out_w, out_b, out):
@@ -35,13 +73,17 @@ def tile_aurelianmemorycore_pb_kernel(tc, h, gated_mem, go_w, go_b, out_w, out_b
     gw_v = go_w.rearrange("(u p e) k -> p u e k", u=2, e=2)
     ow_v = out_w.rearrange("(v p e) k -> p v e k", p=P, e=2)
     out_v = out.flatten_outer_dims().rearrange("(p t) d -> p t d", t=4)
+    group_of = {}
+    for gi, tiles in enumerate(GROUPS):
+        for i, tt in enumerate(tiles):
+            group_of[tt] = (gi, i)
 
     with ExitStack() as ctx:
         keep = ctx.enter_context(tc.tile_pool(name="keep", bufs=1))
         grp = ctx.enter_context(tc.tile_pool(name="grp", bufs=N_GROUPED))
         prod = ctx.enter_context(tc.tile_pool(name="prod", bufs=2))
         banks = ctx.enter_context(tc.psum_pool(name="banks", bufs=N_BANKS))
-        ps1 = ctx.enter_context(tc.psum_pool(name="ps1", bufs=4))
+        ps1 = ctx.enter_context(tc.psum_pool(name="ps1", bufs=N_ACC1))
         if MANUAL:
             ctx.enter_context(tc.manual_schedule())
 
@@ -57,44 +99,66 @@ def tile_aurelianmemorycore_pb_kernel(tc, h, gated_mem, go_w, go_b, out_w, out_b
         make_identity(nc, ident[:])
         nc.scalar.activation(out=warm[:, 1:2], in_=warm[:, 0:1], func=SIGMOID)
 
-        h_a = [keep.tile([P, 2, 1024], BF16, name="h_a%d" % i) for i in range(2)]
-        g_a = keep.tile([P, 2, M], BF16)
+        h_sb = {}
+        g_sb = {}
         gw_cols = ((0, 1024), (1024, 2048), (2048, K1))
-        gw_sb = [[keep.tile([P, 2, hi - lo], BF16, name="gw_sb%d_%d" % (um, lo)) for (lo, hi) in gw_cols] for um in range(2)]
-        ow_sb = [keep.tile([P, 2, 2, M], BF16, name="ow_sb%d" % q) for q in range(4)]
-        g_b = keep.tile([P, 2, M], BF16)
-        h_b = [keep.tile([P, D], BF16, name="h_b%d" % i) for i in range(2)]
-        nc.sync.dma_start(out=h_a[0][:], in_=h_v[:, 0:2, 0:1024])
-        nc.sync.dma_start(out=zrow[0:1, :], in_=out_b.rearrange("(o d) -> o d", o=1))
-        nc.sync.dma_start(out=zb[0:2, :], in_=go_b.rearrange("(u x) -> u x", u=2))
-        nc.sync.dma_start(out=h_a[1][:], in_=h_v[:, 0:2, 1024:2048])
-        nc.sync.dma_start(out=g_a[:], in_=g_v[:, 0:2, :])
-        for i, (lo, hi) in enumerate(gw_cols):
-            for um in range(2):
-                nc.sync.dma_start(out=gw_sb[um][i][:], in_=gw_v[:, um, :, lo:hi])
-        for q in range(4):
-            nc.sync.dma_start(out=ow_sb[q][:], in_=ow_v[:, 2 * q : 2 * q + 2, :, :])
-        nc.sync.dma_start(out=g_b[:], in_=g_v[:, 2:4, :])
-        for i in range(2):
-            nc.sync.dma_start(out=h_b[i][:], in_=h_v[:, 2 + i, :])
+        gw_sb = {}
+        ow_sb = {}
+        for name in LOADS:
+            kind = name[0]
+            if kind == "h":
+                gi = int(name[1])
+                tiles = GROUPS[gi]
+                n = len(tiles)
+                if len(name) == 3:
+                    half = 0 if name[2] == "a" else 1
+                    t = keep.tile([P, n, 1024], BF16, name="h_sb" + name)
+                    nc.sync.dma_start(out=t[:], in_=h_v[:, tiles[0] : tiles[0] + n, 1024 * half : 1024 * half + 1024])
+                    h_sb[(gi, half)] = t
+                else:
+                    t = keep.tile([P, n, D], BF16, name="h_sb" + name)
+                    nc.sync.dma_start(out=t[:], in_=h_v[:, tiles[0] : tiles[0] + n, :])
+                    h_sb[(gi, 2)] = t
+            elif kind == "g" and name != "gb":
+                gi = int(name[1])
+                tiles = GROUPS[gi]
+                t = keep.tile([P, len(tiles), M], BF16, name="g_sb" + name)
+                nc.sync.dma_start(out=t[:], in_=g_v[:, tiles[0] : tiles[0] + len(tiles), :])
+                g_sb[gi] = t
+            elif kind == "w":
+                i, um = int(name[1]), int(name[2])
+                lo, hi = gw_cols[i]
+                t = keep.tile([P, 2, hi - lo], BF16, name="gw_sb" + name)
+                nc.sync.dma_start(out=t[:], in_=gw_v[:, um, :, lo:hi])
+                gw_sb[(um, i)] = t
+            elif kind == "o" and name != "ob":
+                q = int(name[1])
+                t = keep.tile([P, 2, 2, M], BF16, name="ow_sb" + name)
+                nc.sync.dma_start(out=t[:], in_=ow_v[:, 2 * q : 2 * q + 2, :, :])
+                ow_sb[q] = t
+            elif name == "ob":
+                nc.sync.dma_start(out=zrow[0:1, :], in_=out_b.rearrange("(o d) -> o d", o=1))
+            else:
+                nc.sync.dma_start(out=zb[0:2, :], in_=go_b.rearrange("(u x) -> u x", u=2))
 
         def h_block(tt, c):
-            if tt < 2:
-                return h_a[c // 2][:, tt, 512 * (c % 2) : 512 * (c % 2) + 512]
-            return h_b[tt - 2][:, 512 * c : 512 * c + 512]
+            gi, i = group_of[tt]
+            if (gi, 2) in h_sb:
+                return h_sb[(gi, 2)][:, i, 512 * c : 512 * c + 512]
+            return h_sb[(gi, c // 2)][:, i, 512 * (c % 2) : 512 * (c % 2) + 512]
 
         def gate_in_block(tt, c):
             if c < 4:
                 return h_block(tt, c)
-            return g_a[:, tt, :] if tt < 2 else g_b[:, tt - 2, :]
+            gi, i = group_of[tt]
+            return g_sb[gi][:, i, :]
 
         def gw_block(um, e, c):
-            return gw_sb[um][c // 2][:, e, 512 * (c % 2) : 512 * (c % 2) + 512]
+            return gw_sb[(um, c // 2)][:, e, 512 * (c % 2) : 512 * (c % 2) + 512]
 
-        gia_c = keep.tile([P, PASSES1 * 256], U32, align_bytes=64)
-        gia_s = keep.tile([P, PASSES1 * 256], U8, align_bytes=64)
-        gib_c = [keep.tile([P, PASSES1 * P], U32, align_bytes=64, name="gib_c%d" % i) for i in range(2)]
-        gib_s = [keep.tile([P, PASSES1 * P], U8, align_bytes=64, name="gib_s%d" % i) for i in range(2)]
+        gi_c = [keep.tile([P, PASSES1 * P * len(t)], U32, align_bytes=64, name="gi_c%d" % i) for i, t in enumerate(GROUPS)]
+        gi_s = [keep.tile([P, PASSES1 * P * len(t)], U8, align_bytes=64, name="gi_s%d" % i) for i, t in enumerate(GROUPS)]
+        sig = [keep.tile([P, 4, P * len(t)], F32, name="sig%d" % i) for i, t in enumerate(GROUPS)]
         gw_c = keep.tile([P, PASSES1 * M], U32, align_bytes=64)
         gw_s = keep.tile([P, PASSES1 * M], U8, align_bytes=64)
         ow_c = keep.tile([P, D], U32, align_bytes=64)
@@ -102,206 +166,209 @@ def tile_aurelianmemorycore_pb_kernel(tc, h, gated_mem, go_w, go_b, out_w, out_b
         p_c = keep.tile([P, TOK], U32, align_bytes=64)
         p_s = keep.tile([P, TOK], U8, align_bytes=64)
         gq = keep.tile([P, 4 * M], BF16, align_bytes=64)
-        sig_a = keep.tile([P, 4, 256], F32)
-        sig_b = [keep.tile([P, 4, P], F32, name="sig_b%d" % i) for i in range(2)]
         hb = [keep.tile([P, D], F32, name="hb%d" % tt) for tt in range(4)]
         bbc = keep.tile([P, D], F32)
         gob = keep.tile([P, 4], F32)
 
-        def biases():
-            for j in range(4):
-                bb = banks.tile([P, 512], F32, tag="bank")
-                nc.tensor.matmul(out=bb[:], lhsT=ones[:], rhs=zrow[:, 512 * j : 512 * j + 512], start=True, stop=True)
-                nc.vector.tensor_copy(out=bbc[:, 512 * j : 512 * j + 512], in_=bb[:])
-            tb = banks.tile([P, P], F32, tag="bank")
-            nc.tensor.transpose(tb[:], zb[:].bitcast(F32), ident[:])
-            nc.vector.tensor_copy(out=gob[:], in_=tb[:, 0:2].bitcast(BF16))
+        tasks = {}
+        default = []
+        live = {}
 
-        def residual(tt, j):
-            eng = nc.gpsimd if (tt, j) in HB_ON_GPSIMD else nc.vector
-            cols = slice(512 * j, 512 * j + 512)
-            eng.tensor_tensor(out=hb[tt][:, cols], in0=h_block(tt, j), in1=bbc[:, cols], op=ADD)
+        def add(key, fn):
+            tasks[key] = fn
+            default.append(key)
 
-        def residual_on_gpsimd():
-            for tt in range(4):
-                for j in range(4):
-                    if (tt, j) in HB_ON_GPSIMD:
-                        residual(tt, j)
+        units = {}
 
-        hb_vector = [(tt, j) for tt in range(4) for j in range(4) if (tt, j) not in HB_ON_GPSIMD]
+        def unit_tasks(u):
+            def t_task():
+                blocks = units[u][0]
+                xt = banks.tile([P, len(blocks), 2, P], F32, tag="bank")
+                for i, src in enumerate(blocks):
+                    words = src.bitcast(F32)
+                    for w in range(2):
+                        nc.tensor.transpose(xt[:, i, w, :], words[:, P * w : P * w + P], ident[:])
+                live[("xt", u)] = xt
 
-        pending = []
-        count = [0]
+            def x_task():
+                blocks, codes, scales, mix, grouped = units[u]
+                a = len(blocks)
+                xt = live[("xt", u)]
+                if grouped is None:
+                    gt = grp.tile([P, 1024], BF16, tag="grp", align_bytes=64)
+                    grouped = gt[:, 0 : 512 * a]
+                gf = grouped.bitcast(F32)
+                if mix:
+                    dst = gf.rearrange("p (r a u) -> p r a u", a=a, u=2)
+                    src_v = xt[:].rearrange("p a u r -> p r a u")
+                else:
+                    dst = gf.rearrange("p (a r u) -> p a r u", a=a, u=2)
+                    src_v = xt[:].rearrange("p a u r -> p a r u")
+                if u in EXIT_ON_VECTOR:
+                    nc.vector.tensor_copy(out=dst, in_=src_v)
+                else:
+                    nc.scalar.copy(out=dst, in_=src_v)
+                live[("g", u)] = grouped
 
-        def flush():
-            while pending:
-                codes, scales, grouped = pending.pop(0)
-                nc.vector.quantize_mx(out=codes.bitcast(FP8X4), scales=scales, in_=grouped)
+            def q_task():
+                blocks, codes, scales, mix, grouped = units[u]
+                nc.vector.quantize_mx(out=codes.bitcast(FP8X4), scales=scales, in_=live[("g", u)])
 
-        def run(blocks, codes, scales, mix=False, grouped=None):
-            a = len(blocks)
-            xt = banks.tile([P, a, 2, P], F32, tag="bank")
-            for i, src in enumerate(blocks):
-                words = src.bitcast(F32)
-                for u in range(2):
-                    nc.tensor.transpose(xt[:, i, u, :], words[:, P * u : P * u + P], ident[:])
-            if grouped is None:
-                gt = grp.tile([P, 1024], BF16, tag="grp", align_bytes=64)
-                grouped = gt[:, 0 : 512 * a]
-            gf = grouped.bitcast(F32)
-            if mix:
-                dst = gf.rearrange("p (r a u) -> p r a u", a=a, u=2)
-                src_v = xt[:].rearrange("p a u r -> p r a u")
-            else:
-                dst = gf.rearrange("p (a r u) -> p a r u", a=a, u=2)
-                src_v = xt[:].rearrange("p a u r -> p a r u")
-            if count[0] in EXIT_ON_VECTOR:
-                nc.vector.tensor_copy(out=dst, in_=src_v)
-            else:
-                nc.scalar.copy(out=dst, in_=src_v)
-            count[0] += 1
-            flush()
-            pending.append((codes, scales, grouped))
+            add(("T", u), t_task)
+            add(("X", u), x_task)
+            add(("Q", u), q_task)
 
-        def run_gia(c):
-            cols = slice(256 * c, 256 * c + 256)
-            run([gate_in_block(0, c), gate_in_block(1, c)], gia_c[:, cols], gia_s[:, cols],
-                grouped=gq[:, 0:1024] if c == 4 else None)
+        def gate_in_units(gi):
+            tiles = GROUPS[gi]
+            n = len(tiles)
+            blocks = [(c, tt) for c in range(PASSES1) for tt in tiles]
+            k = 0
+            while k < len(blocks):
+                take = blocks[k : k + 2]
+                if take[0][0] < 4 and take[-1][0] == 4:
+                    take = take[:1]
+                cols = slice(P * k, P * k + P * len(take))
+                grouped = None
+                if take[0][0] == 4:
+                    grouped = gq[:, 512 * take[0][1] : 512 * take[0][1] + 512 * len(take)]
+                u = "i%d_%d" % (gi, k)
+                units[u] = ([gate_in_block(tt, c) for c, tt in take], gi_c[gi][:, cols], gi_s[gi][:, cols], False, grouped)
+                unit_tasks(u)
+                k += len(take)
 
-        def run_gw(um, c):
+        def gw_unit(um, c):
             cols = slice(512 * c + 256 * um, 512 * c + 256 * um + 256)
-            run([gw_block(um, 0, c), gw_block(um, 1, c)], gw_c[:, cols], gw_s[:, cols])
+            u = "w%d_%d" % (um, c)
+            units[u] = ([gw_block(um, 0, c), gw_block(um, 1, c)], gw_c[:, cols], gw_s[:, cols], False, None)
+            unit_tasks(u)
 
-        def run_ow(v):
+        def ow_unit(v):
             cols = slice(256 * v, 256 * v + 256)
-            run([ow_sb[v // 2][:, v % 2, 0, :], ow_sb[v // 2][:, v % 2, 1, :]], ow_c[:, cols], ow_s[:, cols], mix=True)
+            u = "o%d" % v
+            units[u] = ([ow_sb[v // 2][:, v % 2, 0, :], ow_sb[v // 2][:, v % 2, 1, :]], ow_c[:, cols], ow_s[:, cols], True, None)
+            unit_tasks(u)
 
-        def run_gib(tt, s):
-            cs = ((0, 1), (2, 3), (4,))[s]
-            cols = slice(P * cs[0], P * cs[0] + P * len(cs))
-            run([gate_in_block(tt, c) for c in cs], gib_c[tt - 2][:, cols], gib_s[tt - 2][:, cols],
-                grouped=gq[:, 512 * tt : 512 * tt + 512] if s == 2 else None)
+        def bias_tasks():
+            for j in range(4):
+                def mm(j=j):
+                    bb = banks.tile([P, 512], F32, tag="bank")
+                    nc.tensor.matmul(out=bb[:], lhsT=ones[:], rhs=zrow[:, 512 * j : 512 * j + 512], start=True, stop=True)
+                    live[("bb", j)] = bb
 
-        def gate(gi_c, gi_s, n, um, sig):
-            acc = ps1.tile([P, 2, n], F32, tag="acc1")
-            for e in range(2):
-                t = 2 * um + e
-                for c in range(PASSES1):
-                    w = slice(512 * c + P * t, 512 * c + P * t + P)
-                    x = slice(n * c, n * c + n)
-                    nc.tensor.matmul_mx(out=acc[:, e, :], lhsT=gw_c[:, w].bitcast(FP8X4), lhsT_scale=gw_s[:, w],
-                                        rhs=gi_c[:, x].bitcast(FP8X4), rhs_scale=gi_s[:, x],
-                                        start=(c == 0), stop=(c == PASSES1 - 1))
-            for e in range(2):
-                t = 2 * um + e
-                nc.scalar.activation(out=sig[:, t, :], in_=acc[:, e, :], func=SIGMOID, bias=gob[:, t : t + 1], scale=1.0)
+                def cp(j=j):
+                    if BIAS_COPY == "v":
+                        nc.vector.tensor_copy(out=bbc[:, 512 * j : 512 * j + 512], in_=live[("bb", j)][:])
+                    else:
+                        nc.scalar.copy(out=bbc[:, 512 * j : 512 * j + 512], in_=live[("bb", j)][:])
 
-        acc_a = []
+                add(("BM", j), mm)
+                add(("BC", j), cp)
 
-        def gate_a_passes(c):
-            if c == 0:
-                for t in range(4):
-                    acc_a.append(ps1.tile([P, 256], F32, tag="acc1", name="acc_a%d" % t))
-            x = slice(256 * c, 256 * c + 256)
+            def gt():
+                tb = banks.tile([P, P], F32, tag="bank")
+                nc.tensor.transpose(tb[:], zb[:].bitcast(F32), ident[:])
+                live["tb"] = tb
+
+            def gc():
+                nc.vector.tensor_copy(out=gob[:], in_=live["tb"][:, 0:2].bitcast(BF16))
+
+            add(("GT", 0), gt)
+            add(("GC", 0), gc)
+
+        def residual_task(tt, j):
+            def fn():
+                eng = nc.gpsimd if (tt, j) in HB_ON_GPSIMD else nc.vector
+                cols = slice(512 * j, 512 * j + 512)
+                eng.tensor_tensor(out=hb[tt][:, cols], in0=h_block(tt, j), in1=bbc[:, cols], op=ADD)
+
+            add(("HB", tt, j), fn)
+
+        def gate_tasks(gi):
+            n = P * len(GROUPS[gi])
+            per_bank = 2 if n <= 256 else 1
             for t in range(4):
-                w = slice(512 * c + P * t, 512 * c + P * t + P)
-                nc.tensor.matmul_mx(out=acc_a[t][:], lhsT=gw_c[:, w].bitcast(FP8X4), lhsT_scale=gw_s[:, w],
-                                    rhs=gia_c[:, x].bitcast(FP8X4), rhs_scale=gia_s[:, x],
-                                    start=(c == 0), stop=(c == PASSES1 - 1))
+                def mx(t=t):
+                    if t % per_bank == 0:
+                        live[("acc", gi, t // per_bank)] = ps1.tile([P, per_bank, n], F32, tag="acc1", name="acc1")
+                    acc = live[("acc", gi, t // per_bank)]
+                    for c in range(PASSES1):
+                        w = slice(512 * c + P * t, 512 * c + P * t + P)
+                        x = slice(n * c, n * c + n)
+                        nc.tensor.matmul_mx(out=acc[:, t % per_bank, :], lhsT=gw_c[:, w].bitcast(FP8X4), lhsT_scale=gw_s[:, w],
+                                            rhs=gi_c[gi][:, x].bitcast(FP8X4), rhs_scale=gi_s[gi][:, x],
+                                            start=(c == 0), stop=(c == PASSES1 - 1))
 
-        def gate_a_sigmoid():
-            for t in range(4):
-                nc.scalar.activation(out=sig_a[:, t, :], in_=acc_a[t][:], func=SIGMOID, bias=gob[:, t : t + 1], scale=1.0)
+                add(("G", gi, t), mx)
+                if t % per_bank == per_bank - 1:
+                    for t2 in range(t - per_bank + 1, t + 1):
+                        def sg(t2=t2):
+                            acc = live[("acc", gi, t2 // per_bank)]
+                            nc.scalar.activation(out=sig[gi][:, t2, :], in_=acc[:, t2 % per_bank, :], func=SIGMOID,
+                                                 bias=gob[:, t2 : t2 + 1], scale=1.0)
 
-        held = {}
+                        add(("S", gi, t2), sg)
 
-        def product(tt):
-            sig = sig_a[:, :, P * tt : P * tt + P] if tt < 2 else sig_b[tt - 2][:]
-            pg = prod.tile([P, 512], BF16, tag="pg", align_bytes=64)
-            nc.vector.tensor_tensor(out=pg[:].rearrange("p (r t) -> p r t", t=4), in0=sig.rearrange("p t r -> p r t"),
-                                    in1=gq[:, 512 * tt : 512 * tt + 512].rearrange("p (r t) -> p r t", t=4), op=MULT)
-            held[tt] = pg
+        def product_tasks(tt):
+            gi, i = group_of[tt]
 
-        def quantise_product(tt):
-            cols = slice(P * tt, P * tt + P)
-            nc.vector.quantize_mx(out=p_c[:, cols].bitcast(FP8X4), scales=p_s[:, cols], in_=held[tt][:])
+            def pr():
+                pg = prod.tile([P, 512], BF16, tag="pg", align_bytes=64)
+                nc.vector.tensor_tensor(out=pg[:].rearrange("p (r t) -> p r t", t=4),
+                                        in0=sig[gi][:, :, P * i : P * i + P].rearrange("p t r -> p r t"),
+                                        in1=gq[:, 512 * tt : 512 * tt + 512].rearrange("p (r t) -> p r t", t=4), op=MULT)
+                live[("pg", tt)] = pg
 
-        def fuse(tt, js):
-            accs = []
-            for j in js:
+            def qp():
+                cols = slice(P * tt, P * tt + P)
+                nc.vector.quantize_mx(out=p_c[:, cols].bitcast(FP8X4), scales=p_s[:, cols], in_=live[("pg", tt)][:])
+
+            add(("PR", tt), pr)
+            add(("QP", tt), qp)
+
+        def fuse_tasks(tt, j):
+            def mx():
                 acc2 = banks.tile([P, 512], F32, tag="bank")
                 t_cols = slice(P * tt, P * tt + P)
                 d_cols = slice(512 * j, 512 * j + 512)
                 nc.tensor.matmul_mx(out=acc2[:], lhsT=p_c[:, t_cols].bitcast(FP8X4), lhsT_scale=p_s[:, t_cols],
                                     rhs=ow_c[:, d_cols].bitcast(FP8X4), rhs_scale=ow_s[:, d_cols], start=True, stop=True)
-                accs.append(acc2)
-            for j, acc2 in zip(js, accs):
+                live[("a2", tt, j)] = acc2
+
+            def fin():
                 d_cols = slice(512 * j, 512 * j + 512)
-                nc.vector.tensor_tensor(out=hb[tt][:, d_cols], in0=acc2[:], in1=hb[tt][:, d_cols], op=ADD)
+                nc.vector.tensor_tensor(out=hb[tt][:, d_cols], in0=live[("a2", tt, j)][:], in1=hb[tt][:, d_cols], op=ADD)
 
-        def store(tt, dh):
-            cols = slice(1024 * dh, 1024 * dh + 1024)
-            nc.sync.dma_start(out=out_v[:, tt, cols], in_=hb[tt][:, cols])
+            add(("F", tt, j), mx)
+            add(("A", tt, j), fin)
 
-        def some_residual(n):
-            for i in range(n):
-                if hb_vector:
-                    tt, j = hb_vector.pop(0)
-                    residual(tt, j)
+        def store_task(tt, dh):
+            def fn():
+                cols = slice(1024 * dh, 1024 * dh + 1024)
+                nc.sync.dma_start(out=out_v[:, tt, cols], in_=hb[tt][:, cols])
 
-        run_gia(0)
-        run_gia(1)
-        flush()
-        biases()
-        residual_on_gpsimd()
-        for c in range(2, PASSES1):
-            run_gia(c)
-            some_residual(1)
+            add(("ST", tt, dh), fn)
+
+        bias_tasks()
+        for tt in range(4):
+            for j in range(4):
+                residual_task(tt, j)
+        gate_in_units(0)
         for c in range(PASSES1):
-            run_gw(0, c)
-            run_gw(1, c)
-            some_residual(1)
-            if c > 0:
-                gate_a_passes(c - 1)
-        run_ow(0)
-        gate_a_passes(PASSES1 - 1)
-        gate_a_sigmoid()
-        flush()
-        some_residual(16)
-        product(0)
-        product(1)
-        quantise_product(0)
-        quantise_product(1)
-        for v in range(1, 5):
-            run_ow(v)
-        fuse(0, (0, 1))
-        store(0, 0)
-        run_ow(5)
-        fuse(1, (0, 1))
-        store(1, 0)
-        run_ow(6)
-        run_ow(7)
-        late = [(tt, s) for tt in (2, 3) for s in range(3)]
-        for tt in (0, 1):
-            b_tt, b_s = late.pop(0)
-            run_gib(b_tt, b_s)
-            fuse(tt, (2, 3))
-            store(tt, 1)
-        for b_tt, b_s in late:
-            run_gib(b_tt, b_s)
-        flush()
-        for tt in (2, 3):
             for um in range(2):
-                gate(gib_c[tt - 2], gib_s[tt - 2], P, um, sig_b[tt - 2])
-        product(2)
-        quantise_product(2)
-        fuse(2, (0,))
-        product(3)
-        quantise_product(3)
-        fuse(2, (1,))
-        store(2, 0)
-        fuse(2, (2, 3))
-        store(2, 1)
-        for dh in (0, 1):
-            fuse(3, (2 * dh, 2 * dh + 1))
-            store(3, dh)
+                gw_unit(um, c)
+        gate_tasks(0)
+        for v in range(8):
+            ow_unit(v)
+        for gi in range(1, len(GROUPS)):
+            gate_in_units(gi)
+            gate_tasks(gi)
+        for tt in range(4):
+            product_tasks(tt)
+            for dh in range(2):
+                for j in (2 * dh, 2 * dh + 1):
+                    fuse_tasks(tt, j)
+                store_task(tt, dh)
+
+        for key in ORDER or default:
+            CURRENT[0] = key
+            tasks[key]()

@@ -13,362 +13,253 @@ MULT = mybir.AluOpType.mult
 SIGMOID = mybir.ActivationFunctionType.Sigmoid
 
 P = 128
-TOK = 512
-D = 2048
-M = 512
-K1 = D + M
-PASSES1 = K1 // 512
+TOKENS = 512
+HIDDEN = 2048
+MEMORY = 512
+K_GATE = HIDDEN + MEMORY
+K_PASS = 4 * P
+GATE_PASSES = K_GATE // K_PASS
+BANK = 512
+TOKEN_TILES = TOKENS // P
+OUT_BANKS = HIDDEN // BANK
 
-FLOPS = 2 * TOK * K1 * M + 2 * TOK * M * D
+FLOPS = 2 * TOKENS * K_GATE * MEMORY + 2 * TOKENS * MEMORY * HIDDEN
 
-CURRENT = [None]
-MANUAL = True
 GROUPS = ((0, 1), (2,), (3,))
-HB_ON_GPSIMD = ((2, 0), (2, 1), (2, 2), (2, 3), (3, 0), (3, 1), (3, 2), (3, 3))
-EXIT_ON_VECTOR = ()
-BIAS_COPY = "v"
-N_BANKS = 6
-N_ACC1 = 2
-N_GROUPED = 6
-LOADS = ("h0a", "ob", "gb", "h0b", "g0", "w00", "w01", "w10", "w11", "w20", "w21", "o0", "o1", "o2", "o3", "g1", "h1", "g2", "h2")
-ORDER = (
-    ("T", "i0_0"), ("GT", 0), ("BM", 0), ("X", "i0_0"), ("GC", 0), ("BM", 1),
-    ("BC", 0), ("BM", 3), ("BM", 2), ("BC", 1), ("T", "i0_2"), ("BC", 3),
-    ("T", "i0_4"), ("X", "i0_2"), ("BC", 2), ("T", "w0_0"), ("X", "i0_4"), ("T", "i0_8"),
-    ("Q", "i0_2"), ("T", "w0_1"), ("X", "w0_0"), ("Q", "i0_0"), ("T", "i0_6"), ("Q", "i0_4"),
-    ("T", "w1_0"), ("X", "i0_8"), ("HB", 0, 0), ("T", "w1_1"), ("X", "i0_6"), ("Q", "w0_0"),
-    ("Q", "i0_8"), ("T", "w0_3"), ("X", "w1_0"), ("HB", 0, 1), ("T", "w0_2"), ("X", "w1_1"),
-    ("Q", "i0_6"), ("T", "w1_3"), ("Q", "w1_0"), ("X", "w0_1"), ("HB", 0, 3), ("T", "w1_2"),
-    ("X", "w0_3"), ("T", "w0_4"), ("Q", "w0_1"), ("Q", "w1_1"), ("T", "w1_4"), ("X", "w0_2"),
-    ("Q", "w0_3"), ("HB", 0, 2), ("X", "w1_3"), ("T", "o0"), ("X", "w1_2"), ("Q", "w0_2"),
-    ("Q", "w1_3"), ("X", "w0_4"), ("HB", 1, 3), ("T", "o1"), ("T", "o2"), ("X", "w1_4"),
-    ("Q", "w1_2"), ("T", "o3"), ("Q", "w0_4"), ("X", "o2"), ("HB", 1, 1), ("G", 0, 0),
-    ("X", "o3"), ("Q", "w1_4"), ("G", 0, 2), ("Q", "o2"), ("X", "o0"), ("HB", 1, 0),
-    ("G", 0, 1), ("X", "o1"), ("Q", "o3"), ("Q", "o0"), ("G", 0, 3), ("HB", 1, 2),
-    ("S", 0, 0), ("S", 0, 1), ("Q", "o1"), ("T", "o4"), ("HB", 2, 0), ("S", 0, 3),
-    ("T", "i1_0"), ("S", 0, 2), ("T", "i1_2"), ("X", "o4"), ("T", "o5"), ("PR", 0),
-    ("HB", 2, 1), ("T", "o6"), ("X", "i1_0"), ("Q", "o4"), ("T", "i1_4"), ("T", "o7"),
-    ("QP", 0), ("X", "i1_2"), ("PR", 1), ("HB", 2, 3), ("X", "o5"), ("F", 0, 0),
-    ("Q", "i1_0"), ("F", 0, 1), ("Q", "i1_2"), ("X", "i1_4"), ("A", 0, 0), ("X", "o6"),
-    ("T", "i2_0"), ("HB", 3, 2), ("Q", "i1_4"), ("G", 1, 2), ("X", "o7"), ("Q", "o5"),
-    ("Q", "o6"), ("X", "i2_0"), ("G", 1, 0), ("A", 0, 1), ("HB", 3, 3), ("G", 1, 1),
-    ("Q", "o7"), ("G", 1, 3), ("ST", 0, 0), ("S", 1, 0), ("Q", "i2_0"), ("F", 0, 2),
-    ("S", 1, 1), ("QP", 1), ("HB", 3, 1), ("S", 1, 2), ("T", "i2_2"), ("S", 1, 3),
-    ("A", 0, 2), ("T", "i2_4"), ("X", "i2_2"), ("F", 0, 3), ("PR", 2), ("F", 1, 2),
-    ("HB", 3, 0), ("X", "i2_4"), ("F", 1, 3), ("A", 0, 3), ("F", 1, 0), ("F", 1, 1),
-    ("Q", "i2_2"), ("HB", 2, 2), ("ST", 0, 1), ("Q", "i2_4"), ("G", 2, 2), ("QP", 2),
-    ("A", 1, 2), ("G", 2, 0), ("A", 1, 3), ("G", 2, 1), ("G", 2, 3), ("A", 1, 1),
-    ("S", 2, 1), ("F", 2, 1), ("S", 2, 0), ("S", 2, 3), ("F", 2, 0), ("A", 1, 0),
-    ("S", 2, 2), ("F", 2, 3), ("PR", 3), ("ST", 1, 0), ("F", 2, 2), ("ST", 1, 1),
-    ("A", 2, 0), ("A", 2, 1), ("QP", 3), ("A", 2, 2), ("ST", 2, 0), ("F", 3, 0),
-    ("A", 2, 3), ("F", 3, 2), ("F", 3, 1), ("A", 3, 0), ("F", 3, 3), ("ST", 2, 1),
-    ("A", 3, 1), ("A", 3, 2), ("ST", 3, 0), ("A", 3, 3), ("ST", 3, 1),
-)
 
 
 def tile_aurelianmemorycore_pb_kernel(tc, h, gated_mem, go_w, go_b, out_w, out_b, out):
     nc = tc.nc
-    h_v = h.flatten_outer_dims().rearrange("(p t) d -> p t d", t=4)
-    g_v = gated_mem.flatten_outer_dims().rearrange("(p t) m -> p t m", t=4)
+    h_v = h.flatten_outer_dims().rearrange("(p i) d -> p i d", i=TOKEN_TILES)
+    g_v = gated_mem.flatten_outer_dims().rearrange("(p i) m -> p i m", i=TOKEN_TILES)
+    out_v = out.flatten_outer_dims().rearrange("(p i) d -> p i d", i=TOKEN_TILES)
     gw_v = go_w.rearrange("(u p e) k -> p u e k", u=2, e=2)
     ow_v = out_w.rearrange("(v p e) k -> p v e k", p=P, e=2)
-    out_v = out.flatten_outer_dims().rearrange("(p t) d -> p t d", t=4)
-    group_of = {}
-    for gi, tiles in enumerate(GROUPS):
-        for i, tt in enumerate(tiles):
-            group_of[tt] = (gi, i)
 
     with ExitStack() as ctx:
         keep = ctx.enter_context(tc.tile_pool(name="keep", bufs=1))
-        grp = ctx.enter_context(tc.tile_pool(name="grp", bufs=N_GROUPED))
-        prod = ctx.enter_context(tc.tile_pool(name="prod", bufs=2))
-        banks = ctx.enter_context(tc.psum_pool(name="banks", bufs=N_BANKS))
-        ps1 = ctx.enter_context(tc.psum_pool(name="ps1", bufs=N_ACC1))
-        if MANUAL:
-            ctx.enter_context(tc.manual_schedule())
+        grouped_pool = ctx.enter_context(tc.tile_pool(name="grouped", bufs=6))
+        product_pool = ctx.enter_context(tc.tile_pool(name="product", bufs=2))
+        banks = ctx.enter_context(tc.psum_pool(name="banks", bufs=6))
+        gate_banks = ctx.enter_context(tc.psum_pool(name="gate_banks", bufs=2))
+        ctx.enter_context(tc.manual_schedule())
 
-        zrow = keep.tile([P, D], BF16)
-        zb = keep.tile([P, 2 * P], BF16)
+        bias_row = keep.tile([P, HIDDEN], BF16)
+        gate_bias_rows = keep.tile([P, 2 * P], BF16)
         ones = keep.tile([P, P], BF16)
-        warm = keep.tile([P, 2], F32)
-        ident = keep.tile([P, P], F32)
-        nc.vector.memset(zrow[:], 0.0)
-        nc.vector.memset(zb[:], 0.0)
+        table_warmer = keep.tile([P, 2], F32)
+        identity = keep.tile([P, P], F32)
+        nc.vector.memset(bias_row[:], 0.0)
+        nc.vector.memset(gate_bias_rows[:], 0.0)
         nc.vector.memset(ones[:], 1.0)
-        nc.vector.memset(warm[:], 0.0)
-        make_identity(nc, ident[:])
-        nc.scalar.activation(out=warm[:, 1:2], in_=warm[:, 0:1], func=SIGMOID)
+        nc.vector.memset(table_warmer[:], 0.0)
+        make_identity(nc, identity[:])
+        nc.scalar.activation(out=table_warmer[:, 1:2], in_=table_warmer[:, 0:1], func=SIGMOID)
 
-        h_sb = {}
-        g_sb = {}
-        gw_cols = ((0, 1024), (1024, 2048), (2048, K1))
-        gw_sb = {}
-        ow_sb = {}
-        for name in LOADS:
-            kind = name[0]
-            if kind == "h":
-                gi = int(name[1])
-                tiles = GROUPS[gi]
-                n = len(tiles)
-                if len(name) == 3:
-                    half = 0 if name[2] == "a" else 1
-                    t = keep.tile([P, n, 1024], BF16, name="h_sb" + name)
-                    nc.sync.dma_start(out=t[:], in_=h_v[:, tiles[0] : tiles[0] + n, 1024 * half : 1024 * half + 1024])
-                    h_sb[(gi, half)] = t
-                else:
-                    t = keep.tile([P, n, D], BF16, name="h_sb" + name)
-                    nc.sync.dma_start(out=t[:], in_=h_v[:, tiles[0] : tiles[0] + n, :])
-                    h_sb[(gi, 2)] = t
-            elif kind == "g" and name != "gb":
-                gi = int(name[1])
-                tiles = GROUPS[gi]
-                t = keep.tile([P, len(tiles), M], BF16, name="g_sb" + name)
-                nc.sync.dma_start(out=t[:], in_=g_v[:, tiles[0] : tiles[0] + len(tiles), :])
-                g_sb[gi] = t
-            elif kind == "w":
-                i, um = int(name[1]), int(name[2])
-                lo, hi = gw_cols[i]
-                t = keep.tile([P, 2, hi - lo], BF16, name="gw_sb" + name)
-                nc.sync.dma_start(out=t[:], in_=gw_v[:, um, :, lo:hi])
-                gw_sb[(um, i)] = t
-            elif kind == "o" and name != "ob":
-                q = int(name[1])
-                t = keep.tile([P, 2, 2, M], BF16, name="ow_sb" + name)
-                nc.sync.dma_start(out=t[:], in_=ow_v[:, 2 * q : 2 * q + 2, :, :])
-                ow_sb[q] = t
-            elif name == "ob":
-                nc.sync.dma_start(out=zrow[0:1, :], in_=out_b.rearrange("(o d) -> o d", o=1))
+        first = len(GROUPS[0])
+        h_first = [keep.tile([P, first, K_PASS], BF16, name="h_first%d" % c) for c in range(2)]
+        h_first.append(keep.tile([P, first, 2 * K_PASS], BF16, name="h_first2"))
+        g_sb = [keep.tile([P, len(tiles), MEMORY], BF16, name="g_sb%d" % g) for g, tiles in enumerate(GROUPS)]
+        h_late = [keep.tile([P, HIDDEN], BF16, name="h_late%d" % g) for g in range(1, len(GROUPS))]
+        gw_chunks = ((0, 1), (2, 3), (4,))
+        gw_sb = [[keep.tile([P, 2, K_PASS * len(cs)], BF16, name="gw_sb%d_%d" % (u, cs[0])) for cs in gw_chunks] for u in range(2)]
+        ow_sb = [keep.tile([P, 2, 2, MEMORY], BF16, name="ow_sb%d" % q) for q in range(4)]
+
+        nc.sync.dma_start(out=h_first[0][:], in_=h_v[:, 0:first, 0:K_PASS])
+        nc.sync.dma_start(out=bias_row[0:1, :], in_=out_b.rearrange("(o d) -> o d", o=1))
+        nc.sync.dma_start(out=gate_bias_rows[0:2, :], in_=go_b.rearrange("(u x) -> u x", u=2))
+        nc.sync.dma_start(out=h_first[1][:], in_=h_v[:, 0:first, K_PASS : 2 * K_PASS])
+        nc.sync.dma_start(out=h_first[2][:], in_=h_v[:, 0:first, 2 * K_PASS : HIDDEN])
+        nc.sync.dma_start(out=g_sb[0][:], in_=g_v[:, 0:first, :])
+        for i, cs in enumerate(gw_chunks):
+            for u in range(2):
+                nc.sync.dma_start(out=gw_sb[u][i][:], in_=gw_v[:, u, :, K_PASS * cs[0] : K_PASS * (cs[-1] + 1)])
+        for q in range(4):
+            nc.sync.dma_start(out=ow_sb[q][:], in_=ow_v[:, 2 * q : 2 * q + 2, :, :])
+        for g in range(1, len(GROUPS)):
+            tile = GROUPS[g][0]
+            nc.sync.dma_start(out=g_sb[g][:], in_=g_v[:, tile : tile + 1, :])
+            nc.sync.dma_start(out=h_late[g - 1][:], in_=h_v[:, tile, :])
+
+        def h_block(tile, c):
+            if tile >= first:
+                return h_late[tile - first][:, K_PASS * c : K_PASS * (c + 1)]
+            if c < 2:
+                return h_first[c][:, tile, :]
+            return h_first[2][:, tile, K_PASS * (c - 2) : K_PASS * (c - 1)]
+
+        def gate_in_block(g, i, c):
+            return h_block(GROUPS[g][i], c) if c < GATE_PASSES - 1 else g_sb[g][:, i, :]
+
+        gi_words = [keep.tile([P, GATE_PASSES * P * len(t)], U32, align_bytes=64, name="gi_words%d" % g) for g, t in enumerate(GROUPS)]
+        gi_scales = [keep.tile([P, GATE_PASSES * P * len(t)], U8, align_bytes=64, name="gi_scales%d" % g) for g, t in enumerate(GROUPS)]
+        gw_words = keep.tile([P, GATE_PASSES * MEMORY], U32, align_bytes=64)
+        gw_scales = keep.tile([P, GATE_PASSES * MEMORY], U8, align_bytes=64)
+        ow_words = keep.tile([P, HIDDEN], U32, align_bytes=64)
+        ow_scales = keep.tile([P, HIDDEN], U8, align_bytes=64)
+        gated_words = keep.tile([P, TOKENS], U32, align_bytes=64)
+        gated_scales = keep.tile([P, TOKENS], U8, align_bytes=64)
+
+        memory_t = keep.tile([P, TOKEN_TILES * MEMORY], BF16, align_bytes=64)
+        gate = [keep.tile([P, 4, P * len(t)], F32, name="gate%d" % g) for g, t in enumerate(GROUPS)]
+        result = [keep.tile([P, HIDDEN], F32, name="result%d" % i) for i in range(TOKEN_TILES)]
+        out_bias = keep.tile([P, HIDDEN], F32)
+        gate_bias = keep.tile([P, 4], F32)
+
+        def make_unit(blocks, words, scales, rows_alternate=False, grouped=None):
+            return {"blocks": blocks, "words": words, "scales": scales, "rows_alternate": rows_alternate, "grouped": grouped}
+
+        def transposes(unit):
+            bank = banks.tile([P, len(unit["blocks"]), 2, P], F32, tag="bank")
+            for a, block in enumerate(unit["blocks"]):
+                pairs = block.bitcast(F32)
+                for u in range(2):
+                    nc.tensor.transpose(bank[:, a, u, :], pairs[:, P * u : P * (u + 1)], identity[:])
+            unit["bank"] = bank
+
+        def copy_out(unit):
+            a = len(unit["blocks"])
+            if unit["grouped"] is None:
+                fresh = grouped_pool.tile([P, 2 * K_PASS], BF16, tag="grouped", align_bytes=64)
+                unit["grouped"] = fresh[:, 0 : K_PASS * a]
+            pairs = unit["grouped"].bitcast(F32)
+            if unit["rows_alternate"]:
+                nc.scalar.copy(out=pairs.rearrange("p (r a u) -> p r a u", a=a, u=2), in_=unit["bank"][:].rearrange("p a u r -> p r a u"))
             else:
-                nc.sync.dma_start(out=zb[0:2, :], in_=go_b.rearrange("(u x) -> u x", u=2))
+                nc.scalar.copy(out=pairs.rearrange("p (a r u) -> p a r u", a=a, u=2), in_=unit["bank"][:].rearrange("p a u r -> p a r u"))
 
-        def h_block(tt, c):
-            gi, i = group_of[tt]
-            if (gi, 2) in h_sb:
-                return h_sb[(gi, 2)][:, i, 512 * c : 512 * c + 512]
-            return h_sb[(gi, c // 2)][:, i, 512 * (c % 2) : 512 * (c % 2) + 512]
+        def quantise(unit):
+            nc.vector.quantize_mx(out=unit["words"].bitcast(FP8X4), scales=unit["scales"], in_=unit["grouped"])
 
-        def gate_in_block(tt, c):
-            if c < 4:
-                return h_block(tt, c)
-            gi, i = group_of[tt]
-            return g_sb[gi][:, i, :]
-
-        def gw_block(um, e, c):
-            return gw_sb[(um, c // 2)][:, e, 512 * (c % 2) : 512 * (c % 2) + 512]
-
-        gi_c = [keep.tile([P, PASSES1 * P * len(t)], U32, align_bytes=64, name="gi_c%d" % i) for i, t in enumerate(GROUPS)]
-        gi_s = [keep.tile([P, PASSES1 * P * len(t)], U8, align_bytes=64, name="gi_s%d" % i) for i, t in enumerate(GROUPS)]
-        sig = [keep.tile([P, 4, P * len(t)], F32, name="sig%d" % i) for i, t in enumerate(GROUPS)]
-        gw_c = keep.tile([P, PASSES1 * M], U32, align_bytes=64)
-        gw_s = keep.tile([P, PASSES1 * M], U8, align_bytes=64)
-        ow_c = keep.tile([P, D], U32, align_bytes=64)
-        ow_s = keep.tile([P, D], U8, align_bytes=64)
-        p_c = keep.tile([P, TOK], U32, align_bytes=64)
-        p_s = keep.tile([P, TOK], U8, align_bytes=64)
-        gq = keep.tile([P, 4 * M], BF16, align_bytes=64)
-        hb = [keep.tile([P, D], F32, name="hb%d" % tt) for tt in range(4)]
-        bbc = keep.tile([P, D], F32)
-        gob = keep.tile([P, 4], F32)
-
-        tasks = {}
-        default = []
-        live = {}
-
-        def add(key, fn):
-            tasks[key] = fn
-            default.append(key)
-
-        units = {}
-
-        def unit_tasks(u):
-            def t_task():
-                blocks = units[u][0]
-                xt = banks.tile([P, len(blocks), 2, P], F32, tag="bank")
-                for i, src in enumerate(blocks):
-                    words = src.bitcast(F32)
-                    for w in range(2):
-                        nc.tensor.transpose(xt[:, i, w, :], words[:, P * w : P * w + P], ident[:])
-                live[("xt", u)] = xt
-
-            def x_task():
-                blocks, codes, scales, mix, grouped = units[u]
-                a = len(blocks)
-                xt = live[("xt", u)]
-                if grouped is None:
-                    gt = grp.tile([P, 1024], BF16, tag="grp", align_bytes=64)
-                    grouped = gt[:, 0 : 512 * a]
-                gf = grouped.bitcast(F32)
-                if mix:
-                    dst = gf.rearrange("p (r a u) -> p r a u", a=a, u=2)
-                    src_v = xt[:].rearrange("p a u r -> p r a u")
-                else:
-                    dst = gf.rearrange("p (a r u) -> p a r u", a=a, u=2)
-                    src_v = xt[:].rearrange("p a u r -> p a r u")
-                if u in EXIT_ON_VECTOR:
-                    nc.vector.tensor_copy(out=dst, in_=src_v)
-                else:
-                    nc.scalar.copy(out=dst, in_=src_v)
-                live[("g", u)] = grouped
-
-            def q_task():
-                blocks, codes, scales, mix, grouped = units[u]
-                nc.vector.quantize_mx(out=codes.bitcast(FP8X4), scales=scales, in_=live[("g", u)])
-
-            add(("T", u), t_task)
-            add(("X", u), x_task)
-            add(("Q", u), q_task)
-
-        def gate_in_units(gi):
-            tiles = GROUPS[gi]
-            n = len(tiles)
-            blocks = [(c, tt) for c in range(PASSES1) for tt in tiles]
-            k = 0
-            while k < len(blocks):
-                take = blocks[k : k + 2]
-                if take[0][0] < 4 and take[-1][0] == 4:
+        def gate_in_units(g):
+            tiles = GROUPS[g]
+            blocks = [(c, i) for c in range(GATE_PASSES) for i in range(len(tiles))]
+            units = []
+            at = 0
+            while at < len(blocks):
+                take = blocks[at : at + 2]
+                if take[0][0] < GATE_PASSES - 1 and take[-1][0] == GATE_PASSES - 1:
                     take = take[:1]
-                cols = slice(P * k, P * k + P * len(take))
+                cols = slice(P * at, P * (at + len(take)))
                 grouped = None
-                if take[0][0] == 4:
-                    grouped = gq[:, 512 * take[0][1] : 512 * take[0][1] + 512 * len(take)]
-                u = "i%d_%d" % (gi, k)
-                units[u] = ([gate_in_block(tt, c) for c, tt in take], gi_c[gi][:, cols], gi_s[gi][:, cols], False, grouped)
-                unit_tasks(u)
-                k += len(take)
+                if take[0][0] == GATE_PASSES - 1:
+                    tile = tiles[take[0][1]]
+                    grouped = memory_t[:, MEMORY * tile : MEMORY * (tile + len(take))]
+                units.append(make_unit([gate_in_block(g, i, c) for c, i in take], gi_words[g][:, cols], gi_scales[g][:, cols], grouped=grouped))
+                at += len(take)
+            return units
 
-        def gw_unit(um, c):
-            cols = slice(512 * c + 256 * um, 512 * c + 256 * um + 256)
-            u = "w%d_%d" % (um, c)
-            units[u] = ([gw_block(um, 0, c), gw_block(um, 1, c)], gw_c[:, cols], gw_s[:, cols], False, None)
-            unit_tasks(u)
+        def gw_unit(u, c):
+            chunk = gw_sb[u][c // 2]
+            k = slice(K_PASS * (c % 2), K_PASS * (c % 2 + 1))
+            cols = slice(MEMORY * c + 2 * P * u, MEMORY * c + 2 * P * (u + 1))
+            return make_unit([chunk[:, 0, k], chunk[:, 1, k]], gw_words[:, cols], gw_scales[:, cols])
 
         def ow_unit(v):
-            cols = slice(256 * v, 256 * v + 256)
-            u = "o%d" % v
-            units[u] = ([ow_sb[v // 2][:, v % 2, 0, :], ow_sb[v // 2][:, v % 2, 1, :]], ow_c[:, cols], ow_s[:, cols], True, None)
-            unit_tasks(u)
+            cols = slice(2 * P * v, 2 * P * (v + 1))
+            rows = ow_sb[v // 2]
+            return make_unit([rows[:, v % 2, 0, :], rows[:, v % 2, 1, :]], ow_words[:, cols], ow_scales[:, cols], rows_alternate=True)
 
-        def bias_tasks():
-            for j in range(4):
-                def mm(j=j):
-                    bb = banks.tile([P, 512], F32, tag="bank")
-                    nc.tensor.matmul(out=bb[:], lhsT=ones[:], rhs=zrow[:, 512 * j : 512 * j + 512], start=True, stop=True)
-                    live[("bb", j)] = bb
+        def spread_biases():
+            rows = []
+            for j in range(OUT_BANKS):
+                bank = banks.tile([P, BANK], F32, tag="bank")
+                nc.tensor.matmul(out=bank[:], lhsT=ones[:], rhs=bias_row[:, BANK * j : BANK * (j + 1)], start=True, stop=True)
+                rows.append(bank)
+            pairs = banks.tile([P, P], F32, tag="bank")
+            nc.tensor.transpose(pairs[:], gate_bias_rows[:].bitcast(F32), identity[:])
+            for j in range(OUT_BANKS):
+                nc.vector.tensor_copy(out=out_bias[:, BANK * j : BANK * (j + 1)], in_=rows[j][:])
+            nc.vector.tensor_copy(out=gate_bias[:], in_=pairs[:, 0:2].bitcast(BF16))
 
-                def cp(j=j):
-                    if BIAS_COPY == "v":
-                        nc.vector.tensor_copy(out=bbc[:, 512 * j : 512 * j + 512], in_=live[("bb", j)][:])
-                    else:
-                        nc.scalar.copy(out=bbc[:, 512 * j : 512 * j + 512], in_=live[("bb", j)][:])
+        def residual(engine, tile, j):
+            cols = slice(BANK * j, BANK * (j + 1))
+            engine.tensor_tensor(out=result[tile][:, cols], in0=h_block(tile, j), in1=out_bias[:, cols], op=ADD)
 
-                add(("BM", j), mm)
-                add(("BC", j), cp)
-
-            def gt():
-                tb = banks.tile([P, P], F32, tag="bank")
-                nc.tensor.transpose(tb[:], zb[:].bitcast(F32), ident[:])
-                live["tb"] = tb
-
-            def gc():
-                nc.vector.tensor_copy(out=gob[:], in_=live["tb"][:, 0:2].bitcast(BF16))
-
-            add(("GT", 0), gt)
-            add(("GC", 0), gc)
-
-        def residual_task(tt, j):
-            def fn():
-                eng = nc.gpsimd if (tt, j) in HB_ON_GPSIMD else nc.vector
-                cols = slice(512 * j, 512 * j + 512)
-                eng.tensor_tensor(out=hb[tt][:, cols], in0=h_block(tt, j), in1=bbc[:, cols], op=ADD)
-
-            add(("HB", tt, j), fn)
-
-        def gate_tasks(gi):
-            n = P * len(GROUPS[gi])
-            per_bank = 2 if n <= 256 else 1
+        def gate_of(g):
+            n = P * len(GROUPS[g])
+            sums = []
             for t in range(4):
-                def mx(t=t):
-                    if t % per_bank == 0:
-                        live[("acc", gi, t // per_bank)] = ps1.tile([P, per_bank, n], F32, tag="acc1", name="acc1")
-                    acc = live[("acc", gi, t // per_bank)]
-                    for c in range(PASSES1):
-                        w = slice(512 * c + P * t, 512 * c + P * t + P)
-                        x = slice(n * c, n * c + n)
-                        nc.tensor.matmul_mx(out=acc[:, t % per_bank, :], lhsT=gw_c[:, w].bitcast(FP8X4), lhsT_scale=gw_s[:, w],
-                                            rhs=gi_c[gi][:, x].bitcast(FP8X4), rhs_scale=gi_s[gi][:, x],
-                                            start=(c == 0), stop=(c == PASSES1 - 1))
+                if t % 2 == 0:
+                    sums.append(gate_banks.tile([P, 2, n], F32, tag="sums", name="sums"))
+                for c in range(GATE_PASSES):
+                    w = slice(MEMORY * c + P * t, MEMORY * c + P * (t + 1))
+                    x = slice(n * c, n * (c + 1))
+                    nc.tensor.matmul_mx(out=sums[t // 2][:, t % 2, :], lhsT=gw_words[:, w].bitcast(FP8X4), lhsT_scale=gw_scales[:, w],
+                                        rhs=gi_words[g][:, x].bitcast(FP8X4), rhs_scale=gi_scales[g][:, x],
+                                        start=(c == 0), stop=(c == GATE_PASSES - 1))
+            for t in range(4):
+                nc.scalar.activation(out=gate[g][:, t, :], in_=sums[t // 2][:, t % 2, :], func=SIGMOID, bias=gate_bias[:, t : t + 1], scale=1.0)
 
-                add(("G", gi, t), mx)
-                if t % per_bank == per_bank - 1:
-                    for t2 in range(t - per_bank + 1, t + 1):
-                        def sg(t2=t2):
-                            acc = live[("acc", gi, t2 // per_bank)]
-                            nc.scalar.activation(out=sig[gi][:, t2, :], in_=acc[:, t2 % per_bank, :], func=SIGMOID,
-                                                 bias=gob[:, t2 : t2 + 1], scale=1.0)
+        gated = {}
 
-                        add(("S", gi, t2), sg)
+        def product(g, i):
+            tile = GROUPS[g][i]
+            gated[tile] = product_pool.tile([P, K_PASS], BF16, tag="gated", name="gated", align_bytes=64)
+            nc.vector.tensor_tensor(out=gated[tile][:].rearrange("p (r t) -> p r t", t=4),
+                                    in0=gate[g][:, :, P * i : P * (i + 1)].rearrange("p t r -> p r t"),
+                                    in1=memory_t[:, MEMORY * tile : MEMORY * (tile + 1)].rearrange("p (r t) -> p r t", t=4), op=MULT)
 
-        def product_tasks(tt):
-            gi, i = group_of[tt]
+        def quantise_product(tile):
+            cols = slice(P * tile, P * (tile + 1))
+            nc.vector.quantize_mx(out=gated_words[:, cols].bitcast(FP8X4), scales=gated_scales[:, cols], in_=gated[tile][:])
 
-            def pr():
-                pg = prod.tile([P, 512], BF16, tag="pg", align_bytes=64)
-                nc.vector.tensor_tensor(out=pg[:].rearrange("p (r t) -> p r t", t=4),
-                                        in0=sig[gi][:, :, P * i : P * i + P].rearrange("p t r -> p r t"),
-                                        in1=gq[:, 512 * tt : 512 * tt + 512].rearrange("p (r t) -> p r t", t=4), op=MULT)
-                live[("pg", tt)] = pg
+        def store(tile, lo, hi):
+            nc.sync.dma_start(out=out_v[:, tile, BANK * lo : BANK * hi], in_=result[tile][:, BANK * lo : BANK * hi])
 
-            def qp():
-                cols = slice(P * tt, P * tt + P)
-                nc.vector.quantize_mx(out=p_c[:, cols].bitcast(FP8X4), scales=p_s[:, cols], in_=live[("pg", tt)][:])
+        def finish(tile, store_each_bank=False):
+            tokens = slice(P * tile, P * (tile + 1))
+            for lo in range(0, OUT_BANKS, 2):
+                products = []
+                for j in (lo, lo + 1):
+                    cols = slice(BANK * j, BANK * (j + 1))
+                    bank = banks.tile([P, BANK], F32, tag="bank")
+                    nc.tensor.matmul_mx(out=bank[:], lhsT=gated_words[:, tokens].bitcast(FP8X4), lhsT_scale=gated_scales[:, tokens],
+                                        rhs=ow_words[:, cols].bitcast(FP8X4), rhs_scale=ow_scales[:, cols], start=True, stop=True)
+                    products.append(bank)
+                for j in (lo, lo + 1):
+                    cols = slice(BANK * j, BANK * (j + 1))
+                    nc.vector.tensor_tensor(out=result[tile][:, cols], in0=products[j - lo][:], in1=result[tile][:, cols], op=ADD)
+                    if store_each_bank and lo > 0:
+                        store(tile, j, j + 1)
+                if not (store_each_bank and lo > 0):
+                    store(tile, lo, lo + 2)
 
-            add(("PR", tt), pr)
-            add(("QP", tt), qp)
+        weights = [gw_unit(u, c) for cs in gw_chunks for u in range(2) for c in cs]
+        projection = [ow_unit(v) for v in range(8)]
+        stream = gate_in_units(0) + weights + projection[:6] + gate_in_units(1) + projection[6:] + gate_in_units(2)
+        first_gate_after = len(GROUPS[0]) * GATE_PASSES // 2 + len(weights) + 3
+        early = [(tile, j) for lo in range(0, OUT_BANKS, 2) for tile in GROUPS[0] for j in (lo, lo + 1)]
 
-        def fuse_tasks(tt, j):
-            def mx():
-                acc2 = banks.tile([P, 512], F32, tag="bank")
-                t_cols = slice(P * tt, P * tt + P)
-                d_cols = slice(512 * j, 512 * j + 512)
-                nc.tensor.matmul_mx(out=acc2[:], lhsT=p_c[:, t_cols].bitcast(FP8X4), lhsT_scale=p_s[:, t_cols],
-                                    rhs=ow_c[:, d_cols].bitcast(FP8X4), rhs_scale=ow_s[:, d_cols], start=True, stop=True)
-                live[("a2", tt, j)] = acc2
+        for n, unit in enumerate(stream):
+            transposes(unit)
+            copy_out(unit)
+            if n > 0 and n != first_gate_after + 1:
+                quantise(stream[n - 1])
+            if n == 0:
+                spread_biases()
+                for tiles in GROUPS[1:]:
+                    for j in range(OUT_BANKS):
+                        residual(nc.gpsimd, tiles[0], j)
+            if n >= 2 and n % 2 == 0 and early:
+                tile, j = early.pop(0)
+                residual(nc.vector, tile, j)
+            if n == first_gate_after:
+                quantise(unit)
+                gate_of(0)
+                product(0, 0)
+                product(0, 1)
+                quantise_product(0)
+                quantise_product(1)
+        quantise(stream[-1])
 
-            def fin():
-                d_cols = slice(512 * j, 512 * j + 512)
-                nc.vector.tensor_tensor(out=hb[tt][:, d_cols], in0=live[("a2", tt, j)][:], in1=hb[tt][:, d_cols], op=ADD)
-
-            add(("F", tt, j), mx)
-            add(("A", tt, j), fin)
-
-        def store_task(tt, dh):
-            def fn():
-                cols = slice(1024 * dh, 1024 * dh + 1024)
-                nc.sync.dma_start(out=out_v[:, tt, cols], in_=hb[tt][:, cols])
-
-            add(("ST", tt, dh), fn)
-
-        bias_tasks()
-        for tt in range(4):
-            for j in range(4):
-                residual_task(tt, j)
-        gate_in_units(0)
-        for c in range(PASSES1):
-            for um in range(2):
-                gw_unit(um, c)
-        gate_tasks(0)
-        for v in range(8):
-            ow_unit(v)
-        for gi in range(1, len(GROUPS)):
-            gate_in_units(gi)
-            gate_tasks(gi)
-        for tt in range(4):
-            product_tasks(tt)
-            for dh in range(2):
-                for j in (2 * dh, 2 * dh + 1):
-                    fuse_tasks(tt, j)
-                store_task(tt, dh)
-
-        for key in ORDER or default:
-            CURRENT[0] = key
-            tasks[key]()
+        gate_of(1)
+        finish(0)
+        product(1, 0)
+        quantise_product(2)
+        gate_of(2)
+        finish(1)
+        product(2, 0)
+        quantise_product(3)
+        finish(2)
+        finish(3, store_each_bank=True)

@@ -57,19 +57,17 @@ def tile_aurelianmemorycore_pb_kernel(tc, h, gated_mem, go_w, go_b, out_w, out_b
         nc.scalar.activation(out=table_warmer[:, 1:2], in_=table_warmer[:, 0:1], func=SIGMOID)
 
         first = len(GROUPS[0])
-        h_first = [keep.tile([P, first, K_PASS], BF16, name="h_first%d" % c) for c in range(2)]
-        h_first.append(keep.tile([P, first, 2 * K_PASS], BF16, name="h_first2"))
+        h_first = [keep.tile([P, first, 2 * K_PASS], BF16, name="h_first%d" % half) for half in range(2)]
         g_sb = [keep.tile([P, len(tiles), MEMORY], BF16, name="g_sb%d" % g) for g, tiles in enumerate(GROUPS)]
         h_late = [keep.tile([P, HIDDEN], BF16, name="h_late%d" % g) for g in range(1, len(GROUPS))]
         gw_chunks = ((0, 1), (2, 3), (4,))
         gw_sb = [[keep.tile([P, 2, K_PASS * len(cs)], BF16, name="gw_sb%d_%d" % (u, cs[0])) for cs in gw_chunks] for u in range(2)]
         ow_sb = [keep.tile([P, 2, 2, MEMORY], BF16, name="ow_sb%d" % q) for q in range(4)]
 
-        nc.sync.dma_start(out=h_first[0][:], in_=h_v[:, 0:first, 0:K_PASS])
+        nc.sync.dma_start(out=h_first[0][:], in_=h_v[:, 0:first, 0 : 2 * K_PASS])
         nc.sync.dma_start(out=bias_row[0:1, :], in_=out_b.rearrange("(o d) -> o d", o=1))
         nc.sync.dma_start(out=gate_bias_rows[0:2, :], in_=go_b.rearrange("(u x) -> u x", u=2))
-        nc.sync.dma_start(out=h_first[1][:], in_=h_v[:, 0:first, K_PASS : 2 * K_PASS])
-        nc.sync.dma_start(out=h_first[2][:], in_=h_v[:, 0:first, 2 * K_PASS : HIDDEN])
+        nc.sync.dma_start(out=h_first[1][:], in_=h_v[:, 0:first, 2 * K_PASS : HIDDEN])
         nc.sync.dma_start(out=g_sb[0][:], in_=g_v[:, 0:first, :])
         for i, cs in enumerate(gw_chunks):
             for u in range(2):
@@ -84,9 +82,7 @@ def tile_aurelianmemorycore_pb_kernel(tc, h, gated_mem, go_w, go_b, out_w, out_b
         def h_block(tile, c):
             if tile >= first:
                 return h_late[tile - first][:, K_PASS * c : K_PASS * (c + 1)]
-            if c < 2:
-                return h_first[c][:, tile, :]
-            return h_first[2][:, tile, K_PASS * (c - 2) : K_PASS * (c - 1)]
+            return h_first[c // 2][:, tile, K_PASS * (c % 2) : K_PASS * (c % 2 + 1)]
 
         def gate_in_block(g, i, c):
             return h_block(GROUPS[g][i], c) if c < GATE_PASSES - 1 else g_sb[g][:, i, :]
@@ -204,38 +200,39 @@ def tile_aurelianmemorycore_pb_kernel(tc, h, gated_mem, go_w, go_b, out_w, out_b
             cols = slice(P * tile, P * (tile + 1))
             nc.vector.quantize_mx(out=gated_words[:, cols].bitcast(FP8X4), scales=gated_scales[:, cols], in_=gated[tile][:])
 
-        def store(tile, lo, hi):
-            nc.sync.dma_start(out=out_v[:, tile, BANK * lo : BANK * hi], in_=result[tile][:, BANK * lo : BANK * hi])
-
-        def finish(tile, store_each_bank=False):
+        def finish_half(tile, lo):
             tokens = slice(P * tile, P * (tile + 1))
-            for lo in range(0, OUT_BANKS, 2):
-                products = []
-                for j in (lo, lo + 1):
-                    cols = slice(BANK * j, BANK * (j + 1))
-                    bank = banks.tile([P, BANK], F32, tag="bank")
-                    nc.tensor.matmul_mx(out=bank[:], lhsT=gated_words[:, tokens].bitcast(FP8X4), lhsT_scale=gated_scales[:, tokens],
-                                        rhs=ow_words[:, cols].bitcast(FP8X4), rhs_scale=ow_scales[:, cols], start=True, stop=True)
-                    products.append(bank)
-                for j in (lo, lo + 1):
-                    cols = slice(BANK * j, BANK * (j + 1))
-                    nc.vector.tensor_tensor(out=result[tile][:, cols], in0=products[j - lo][:], in1=result[tile][:, cols], op=ADD)
-                    if store_each_bank and lo > 0:
-                        store(tile, j, j + 1)
-                if not (store_each_bank and lo > 0):
-                    store(tile, lo, lo + 2)
+            products = []
+            for j in (lo, lo + 1):
+                cols = slice(BANK * j, BANK * (j + 1))
+                bank = banks.tile([P, BANK], F32, tag="bank")
+                nc.tensor.matmul_mx(out=bank[:], lhsT=gated_words[:, tokens].bitcast(FP8X4), lhsT_scale=gated_scales[:, tokens],
+                                    rhs=ow_words[:, cols].bitcast(FP8X4), rhs_scale=ow_scales[:, cols], start=True, stop=True)
+                products.append(bank)
+            for j in (lo, lo + 1):
+                cols = slice(BANK * j, BANK * (j + 1))
+                nc.vector.tensor_tensor(out=result[tile][:, cols], in0=products[j - lo][:], in1=result[tile][:, cols], op=ADD)
+            nc.sync.dma_start(out=out_v[:, tile, BANK * lo : BANK * (lo + 2)], in_=result[tile][:, BANK * lo : BANK * (lo + 2)])
+
+        copied = []
+
+        def catch_up():
+            if copied:
+                quantise(copied.pop())
+
+        def prepare(unit):
+            transposes(unit)
+            copy_out(unit)
+            catch_up()
+            copied.append(unit)
 
         weights = [gw_unit(u, c) for cs in gw_chunks for u in range(2) for c in cs]
         projection = [ow_unit(v) for v in range(8)]
-        stream = gate_in_units(0) + weights + projection[:6] + gate_in_units(1) + projection[6:] + gate_in_units(2)
-        first_gate_after = len(GROUPS[0]) * GATE_PASSES // 2 + len(weights) + 3
+        second, third = gate_in_units(1), gate_in_units(2)
         early = [(tile, j) for lo in range(0, OUT_BANKS, 2) for tile in GROUPS[0] for j in (lo, lo + 1)]
 
-        for n, unit in enumerate(stream):
-            transposes(unit)
-            copy_out(unit)
-            if n > 0 and n != first_gate_after + 1:
-                quantise(stream[n - 1])
+        for n, unit in enumerate(gate_in_units(0) + weights + projection[:4]):
+            prepare(unit)
             if n == 0:
                 spread_biases()
                 for tiles in GROUPS[1:]:
@@ -244,22 +241,31 @@ def tile_aurelianmemorycore_pb_kernel(tc, h, gated_mem, go_w, go_b, out_w, out_b
             if n >= 2 and n % 2 == 0 and early:
                 tile, j = early.pop(0)
                 residual(nc.vector, tile, j)
-            if n == first_gate_after:
-                quantise(unit)
-                gate_of(0)
-                product(0, 0)
-                product(0, 1)
-                quantise_product(0)
-                quantise_product(1)
-        quantise(stream[-1])
-
+        catch_up()
+        gate_of(0)
+        product(0, 0)
+        product(0, 1)
+        quantise_product(0)
+        quantise_product(1)
+        for k in range(4):
+            prepare(projection[4 + k])
+            if k < len(second):
+                prepare(second[k])
+        catch_up()
+        finish_half(0, 0)
+        prepare(third[0])
         gate_of(1)
-        finish(0)
+        finish_half(0, 2)
+        prepare(third[1])
+        prepare(third[2])
+        catch_up()
         product(1, 0)
         quantise_product(2)
+        finish_half(1, 0)
+        finish_half(1, 2)
         gate_of(2)
-        finish(1)
         product(2, 0)
         quantise_product(3)
-        finish(2)
-        finish(3, store_each_bank=True)
+        for tile in (2, 3):
+            finish_half(tile, 0)
+            finish_half(tile, 2)

@@ -42,7 +42,6 @@ def tile_aurelianmemorycore_pb_kernel(tc, h, gated_mem, go_w, go_b, out_w, out_b
         product_pool = ctx.enter_context(tc.tile_pool(name="product", bufs=2))
         banks = ctx.enter_context(tc.psum_pool(name="banks", bufs=6))
         gate_banks = ctx.enter_context(tc.psum_pool(name="gate_banks", bufs=2))
-        ctx.enter_context(tc.manual_schedule())
 
         bias_row = keep.tile([P, HIDDEN], BF16)
         gate_bias_rows = keep.tile([P, 2 * P], BF16)

@@ -25,8 +25,6 @@ OUT_BANKS = HIDDEN // BANK
 
 FLOPS = 2 * TOKENS * K_GATE * MEMORY + 2 * TOKENS * MEMORY * HIDDEN
 
-GROUPS = ((0, 1), (2,), (3,))
-
 
 def tile_aurelianmemorycore_pb_kernel(tc, h, gated_mem, go_w, go_b, out_w, out_b, out):
     nc = tc.nc
@@ -34,12 +32,12 @@ def tile_aurelianmemorycore_pb_kernel(tc, h, gated_mem, go_w, go_b, out_w, out_b
     g_v = gated_mem.flatten_outer_dims().rearrange("(p i) m -> p i m", i=TOKEN_TILES)
     out_v = out.flatten_outer_dims().rearrange("(p i) d -> p i d", i=TOKEN_TILES)
     gw_v = go_w.rearrange("(u p e) k -> p u e k", u=2, e=2)
-    ow_v = out_w.rearrange("(v p e) k -> p v e k", p=P, e=2)
+    ow_v = out_w.rearrange("(j p x) k -> p j x k", j=OUT_BANKS, x=4)
 
     with ExitStack() as ctx:
         keep = ctx.enter_context(tc.tile_pool(name="keep", bufs=1))
         grouped_pool = ctx.enter_context(tc.tile_pool(name="grouped", bufs=6))
-        product_pool = ctx.enter_context(tc.tile_pool(name="product", bufs=2))
+        product_pool = ctx.enter_context(tc.tile_pool(name="product", bufs=4))
         banks = ctx.enter_context(tc.psum_pool(name="banks", bufs=6))
         gate_banks = ctx.enter_context(tc.psum_pool(name="gate_banks", bufs=2))
 
@@ -48,46 +46,40 @@ def tile_aurelianmemorycore_pb_kernel(tc, h, gated_mem, go_w, go_b, out_w, out_b
         ones = keep.tile([P, P], BF16)
         table_warmer = keep.tile([P, 2], F32)
         identity = keep.tile([P, P], F32)
-        nc.vector.memset(bias_row[:], 0.0)
+        identity_bf = keep.tile([P, P], BF16)
+        nc.vector.memset(table_warmer[:], 0.0)
         nc.vector.memset(gate_bias_rows[:], 0.0)
         nc.vector.memset(ones[:], 1.0)
-        nc.vector.memset(table_warmer[:], 0.0)
         make_identity(nc, identity[:])
+        nc.vector.memset(bias_row[:].bitcast(U32), 0)
+        nc.vector.tensor_copy(out=identity_bf[:], in_=identity[:])
         nc.scalar.activation(out=table_warmer[:, 1:2], in_=table_warmer[:, 0:1], func=SIGMOID)
 
-        first = len(GROUPS[0])
-        h_first = [keep.tile([P, first, 2 * K_PASS], BF16, name="h_first%d" % half) for half in range(2)]
-        g_sb = [keep.tile([P, len(tiles), MEMORY], BF16, name="g_sb%d" % g) for g, tiles in enumerate(GROUPS)]
-        h_late = [keep.tile([P, HIDDEN], BF16, name="h_late%d" % g) for g in range(1, len(GROUPS))]
-        gw_chunks = ((0, 1), (2, 3), (4,))
-        gw_sb = [[keep.tile([P, 2, K_PASS * len(cs)], BF16, name="gw_sb%d_%d" % (u, cs[0])) for cs in gw_chunks] for u in range(2)]
-        ow_sb = [keep.tile([P, 2, 2, MEMORY], BF16, name="ow_sb%d" % q) for q in range(4)]
+        h_sb = [[keep.tile([P, 2, 2 * K_PASS], BF16, name="h_sb%d_%d" % (half, pair)) for pair in range(2)] for half in range(2)]
+        g_sb = keep.tile([P, TOKEN_TILES, MEMORY], BF16)
+        gw_sb = [keep.tile([P, K_GATE], BF16, name="gw_sb%d" % t) for t in range(4)]
+        ow_sb = [keep.tile([P, 4, MEMORY], BF16, name="ow_sb%d" % j) for j in range(OUT_BANKS)]
 
-        nc.sync.dma_start(out=h_first[0][:], in_=h_v[:, 0:first, 0 : 2 * K_PASS])
+        def load_h(half, pair):
+            nc.sync.dma_start(out=h_sb[half][pair][:], in_=h_v[:, 2 * pair : 2 * pair + 2, 2 * K_PASS * half : 2 * K_PASS * (half + 1)])
+
+        load_h(0, 0)
+        load_h(0, 1)
         nc.sync.dma_start(out=bias_row[0:1, :], in_=out_b.rearrange("(o d) -> o d", o=1))
         nc.sync.dma_start(out=gate_bias_rows[0:2, :], in_=go_b.rearrange("(u x) -> u x", u=2))
-        nc.sync.dma_start(out=h_first[1][:], in_=h_v[:, 0:first, 2 * K_PASS : HIDDEN])
-        nc.sync.dma_start(out=g_sb[0][:], in_=g_v[:, 0:first, :])
-        for i, cs in enumerate(gw_chunks):
-            for u in range(2):
-                nc.sync.dma_start(out=gw_sb[u][i][:], in_=gw_v[:, u, :, K_PASS * cs[0] : K_PASS * (cs[-1] + 1)])
-        for q in range(4):
-            nc.sync.dma_start(out=ow_sb[q][:], in_=ow_v[:, 2 * q : 2 * q + 2, :, :])
-        for g in range(1, len(GROUPS)):
-            tile = GROUPS[g][0]
-            nc.sync.dma_start(out=g_sb[g][:], in_=g_v[:, tile : tile + 1, :])
-            nc.sync.dma_start(out=h_late[g - 1][:], in_=h_v[:, tile, :])
+        load_h(1, 0)
+        load_h(1, 1)
+        nc.sync.dma_start(out=g_sb[:], in_=g_v)
+        for t in range(4):
+            nc.sync.dma_start(out=gw_sb[t][:], in_=gw_v[:, t // 2, t % 2, :])
+        for j in range(OUT_BANKS):
+            nc.sync.dma_start(out=ow_sb[j][:], in_=ow_v[:, j, :, :])
 
         def h_block(tile, c):
-            if tile >= first:
-                return h_late[tile - first][:, K_PASS * c : K_PASS * (c + 1)]
-            return h_first[c // 2][:, tile, K_PASS * (c % 2) : K_PASS * (c % 2 + 1)]
+            return h_sb[c // 2][tile // 2][:, tile % 2, K_PASS * (c % 2) : K_PASS * (c % 2 + 1)]
 
-        def gate_in_block(g, i, c):
-            return h_block(GROUPS[g][i], c) if c < GATE_PASSES - 1 else g_sb[g][:, i, :]
-
-        gi_words = [keep.tile([P, GATE_PASSES * P * len(t)], U32, align_bytes=64, name="gi_words%d" % g) for g, t in enumerate(GROUPS)]
-        gi_scales = [keep.tile([P, GATE_PASSES * P * len(t)], U8, align_bytes=64, name="gi_scales%d" % g) for g, t in enumerate(GROUPS)]
+        gi_words = keep.tile([P, GATE_PASSES * TOKENS], U32, align_bytes=64)
+        gi_scales = keep.tile([P, GATE_PASSES * TOKENS], U8, align_bytes=64)
         gw_words = keep.tile([P, GATE_PASSES * MEMORY], U32, align_bytes=64)
         gw_scales = keep.tile([P, GATE_PASSES * MEMORY], U8, align_bytes=64)
         ow_words = keep.tile([P, HIDDEN], U32, align_bytes=64)
@@ -96,16 +88,15 @@ def tile_aurelianmemorycore_pb_kernel(tc, h, gated_mem, go_w, go_b, out_w, out_b
         gated_scales = keep.tile([P, TOKENS], U8, align_bytes=64)
 
         memory_t = keep.tile([P, TOKEN_TILES * MEMORY], BF16, align_bytes=64)
-        gate = [keep.tile([P, 4, P * len(t)], F32, name="gate%d" % g) for g, t in enumerate(GROUPS)]
+        gate = keep.tile([P, 4, TOKENS], F32)
         result = [keep.tile([P, HIDDEN], F32, name="result%d" % i) for i in range(TOKEN_TILES)]
-        out_bias = keep.tile([P, HIDDEN], F32)
         gate_bias = keep.tile([P, 4], F32)
 
-        def make_unit(blocks, words, scales, rows_alternate=False, grouped=None):
-            return {"blocks": blocks, "words": words, "scales": scales, "rows_alternate": rows_alternate, "grouped": grouped}
+        def make_unit(blocks, words, scales, grouped=None):
+            return {"blocks": blocks, "words": words, "scales": scales, "grouped": grouped}
 
         def transposes(unit):
-            bank = banks.tile([P, len(unit["blocks"]), 2, P], F32, tag="bank")
+            bank = banks.tile([P, 2, 2, P], F32, tag="bank")
             for a, block in enumerate(unit["blocks"]):
                 pairs = block.bitcast(F32)
                 for u in range(2):
@@ -113,105 +104,88 @@ def tile_aurelianmemorycore_pb_kernel(tc, h, gated_mem, go_w, go_b, out_w, out_b
             unit["bank"] = bank
 
         def copy_out(unit):
-            a = len(unit["blocks"])
             if unit["grouped"] is None:
                 fresh = grouped_pool.tile([P, 2 * K_PASS], BF16, tag="grouped", align_bytes=64)
-                unit["grouped"] = fresh[:, 0 : K_PASS * a]
+                unit["grouped"] = fresh[:]
             pairs = unit["grouped"].bitcast(F32)
-            if unit["rows_alternate"]:
-                nc.scalar.copy(out=pairs.rearrange("p (r a u) -> p r a u", a=a, u=2), in_=unit["bank"][:].rearrange("p a u r -> p r a u"))
-            else:
-                nc.scalar.copy(out=pairs.rearrange("p (a r u) -> p a r u", a=a, u=2), in_=unit["bank"][:].rearrange("p a u r -> p a r u"))
+            nc.scalar.copy(out=pairs.rearrange("p (a r u) -> p a r u", a=2, u=2), in_=unit["bank"][:].rearrange("p a u r -> p a r u"))
 
         def quantise(unit):
             nc.vector.quantize_mx(out=unit["words"].bitcast(FP8X4), scales=unit["scales"], in_=unit["grouped"])
 
-        def gate_in_units(g):
-            tiles = GROUPS[g]
-            blocks = [(c, i) for c in range(GATE_PASSES) for i in range(len(tiles))]
-            units = []
-            at = 0
-            while at < len(blocks):
-                take = blocks[at : at + 2]
-                if take[0][0] < GATE_PASSES - 1 and take[-1][0] == GATE_PASSES - 1:
-                    take = take[:1]
-                cols = slice(P * at, P * (at + len(take)))
-                grouped = None
-                if take[0][0] == GATE_PASSES - 1:
-                    tile = tiles[take[0][1]]
-                    grouped = memory_t[:, MEMORY * tile : MEMORY * (tile + len(take))]
-                units.append(make_unit([gate_in_block(g, i, c) for c, i in take], gi_words[g][:, cols], gi_scales[g][:, cols], grouped=grouped))
-                at += len(take)
-            return units
+        def gi_unit(c, pair):
+            cols = slice(TOKENS * c + 2 * P * pair, TOKENS * c + 2 * P * (pair + 1))
+            if c < GATE_PASSES - 1:
+                return make_unit([h_block(2 * pair, c), h_block(2 * pair + 1, c)], gi_words[:, cols], gi_scales[:, cols])
+            return make_unit([g_sb[:, 2 * pair, :], g_sb[:, 2 * pair + 1, :]], gi_words[:, cols], gi_scales[:, cols],
+                             grouped=memory_t[:, 2 * MEMORY * pair : 2 * MEMORY * (pair + 1)])
 
-        def gw_unit(u, c):
-            chunk = gw_sb[u][c // 2]
-            k = slice(K_PASS * (c % 2), K_PASS * (c % 2 + 1))
-            cols = slice(MEMORY * c + 2 * P * u, MEMORY * c + 2 * P * (u + 1))
-            return make_unit([chunk[:, 0, k], chunk[:, 1, k]], gw_words[:, cols], gw_scales[:, cols])
+        def gw_unit(n):
+            cols = slice(2 * P * n, 2 * P * (n + 1))
+            blocks = []
+            for b in (2 * n, 2 * n + 1):
+                t, c = divmod(b, GATE_PASSES)
+                blocks.append(gw_sb[t][:, K_PASS * c : K_PASS * (c + 1)])
+            return make_unit(blocks, gw_words[:, cols], gw_scales[:, cols])
 
-        def ow_unit(v):
-            cols = slice(2 * P * v, 2 * P * (v + 1))
-            rows = ow_sb[v // 2]
-            return make_unit([rows[:, v % 2, 0, :], rows[:, v % 2, 1, :]], ow_words[:, cols], ow_scales[:, cols], rows_alternate=True)
+        def ow_unit(j, y):
+            cols = slice(BANK * j + 2 * P * y, BANK * j + 2 * P * (y + 1))
+            return make_unit([ow_sb[j][:, 2 * y, :], ow_sb[j][:, 2 * y + 1, :]], ow_words[:, cols], ow_scales[:, cols])
 
-        def spread_biases():
-            rows = []
-            for j in range(OUT_BANKS):
-                bank = banks.tile([P, BANK], F32, tag="bank")
-                nc.tensor.matmul(out=bank[:], lhsT=ones[:], rhs=bias_row[:, BANK * j : BANK * (j + 1)], start=True, stop=True)
-                rows.append(bank)
+        bias_banks = {}
+
+        def spread_bias(j):
+            bank = banks.tile([P, BANK], F32, tag="bank")
+            nc.tensor.matmul(out=bank[:], lhsT=ones[:], rhs=bias_row[:, BANK * j : BANK * (j + 1)], start=True, stop=True)
+            bias_banks[j] = bank
+
+        def residual_vector(tile, j):
+            cols = slice(BANK * j, BANK * (j + 1))
+            nc.vector.tensor_tensor(out=result[tile][:, cols], in0=bias_banks[j][:], in1=h_block(tile, j), op=ADD)
+
+        def residual_tensor(tile, j):
+            cols = slice(BANK * j, BANK * (j + 1))
+            bank = banks.tile([P, BANK], F32, tag="bank")
+            nc.tensor.matmul(out=bank[:], lhsT=identity_bf[:], rhs=h_block(tile, j), start=True, stop=False)
+            nc.tensor.matmul(out=bank[:], lhsT=ones[:], rhs=bias_row[:, cols], start=False, stop=True)
+            nc.scalar.copy(out=result[tile][:, cols], in_=bank[:])
+
+        def spread_gate_bias():
             pairs = banks.tile([P, P], F32, tag="bank")
             nc.tensor.transpose(pairs[:], gate_bias_rows[:].bitcast(F32), identity[:])
-            for j in range(OUT_BANKS):
-                nc.vector.tensor_copy(out=out_bias[:, BANK * j : BANK * (j + 1)], in_=rows[j][:])
             nc.vector.tensor_copy(out=gate_bias[:], in_=pairs[:, 0:2].bitcast(BF16))
 
-        def residual(engine, tile, j):
-            cols = slice(BANK * j, BANK * (j + 1))
-            engine.tensor_tensor(out=result[tile][:, cols], in0=h_block(tile, j), in1=out_bias[:, cols], op=ADD)
-
-        def gate_of(g):
-            n = P * len(GROUPS[g])
-            sums = []
-            for t in range(4):
-                if t % 2 == 0:
-                    sums.append(gate_banks.tile([P, 2, n], F32, tag="sums", name="sums"))
-                for c in range(GATE_PASSES):
-                    w = slice(MEMORY * c + P * t, MEMORY * c + P * (t + 1))
-                    x = slice(n * c, n * (c + 1))
-                    nc.tensor.matmul_mx(out=sums[t // 2][:, t % 2, :], lhsT=gw_words[:, w].bitcast(FP8X4), lhsT_scale=gw_scales[:, w],
-                                        rhs=gi_words[g][:, x].bitcast(FP8X4), rhs_scale=gi_scales[g][:, x],
-                                        start=(c == 0), stop=(c == GATE_PASSES - 1))
-            for t in range(4):
-                nc.scalar.activation(out=gate[g][:, t, :], in_=sums[t // 2][:, t % 2, :], func=SIGMOID, bias=gate_bias[:, t : t + 1], scale=1.0)
+        def gate_of(t):
+            sums = gate_banks.tile([P, TOKENS], F32, tag="sums", name="sums")
+            for c in range(GATE_PASSES):
+                w = slice(P * (GATE_PASSES * t + c), P * (GATE_PASSES * t + c + 1))
+                x = slice(TOKENS * c, TOKENS * (c + 1))
+                nc.tensor.matmul_mx(out=sums[:], lhsT=gw_words[:, w].bitcast(FP8X4), lhsT_scale=gw_scales[:, w],
+                                    rhs=gi_words[:, x].bitcast(FP8X4), rhs_scale=gi_scales[:, x],
+                                    start=(c == 0), stop=(c == GATE_PASSES - 1))
+            nc.scalar.activation(out=gate[:, t, :], in_=sums[:], func=SIGMOID, bias=gate_bias[:, t : t + 1], scale=1.0)
 
         gated = {}
 
-        def product(g, i):
-            tile = GROUPS[g][i]
+        def product(tile):
             gated[tile] = product_pool.tile([P, K_PASS], BF16, tag="gated", name="gated", align_bytes=64)
             nc.vector.tensor_tensor(out=gated[tile][:].rearrange("p (r t) -> p r t", t=4),
-                                    in0=gate[g][:, :, P * i : P * (i + 1)].rearrange("p t r -> p r t"),
+                                    in0=gate[:, :, P * tile : P * (tile + 1)].rearrange("p t r -> p r t"),
                                     in1=memory_t[:, MEMORY * tile : MEMORY * (tile + 1)].rearrange("p (r t) -> p r t", t=4), op=MULT)
 
         def quantise_product(tile):
             cols = slice(P * tile, P * (tile + 1))
             nc.vector.quantize_mx(out=gated_words[:, cols].bitcast(FP8X4), scales=gated_scales[:, cols], in_=gated[tile][:])
 
-        def finish_half(tile, lo):
+        def finish(tile, j):
             tokens = slice(P * tile, P * (tile + 1))
-            products = []
-            for j in (lo, lo + 1):
-                cols = slice(BANK * j, BANK * (j + 1))
-                bank = banks.tile([P, BANK], F32, tag="bank")
-                nc.tensor.matmul_mx(out=bank[:], lhsT=gated_words[:, tokens].bitcast(FP8X4), lhsT_scale=gated_scales[:, tokens],
-                                    rhs=ow_words[:, cols].bitcast(FP8X4), rhs_scale=ow_scales[:, cols], start=True, stop=True)
-                products.append(bank)
-            for j in (lo, lo + 1):
-                cols = slice(BANK * j, BANK * (j + 1))
-                nc.vector.tensor_tensor(out=result[tile][:, cols], in0=products[j - lo][:], in1=result[tile][:, cols], op=ADD)
-            nc.sync.dma_start(out=out_v[:, tile, BANK * lo : BANK * (lo + 2)], in_=result[tile][:, BANK * lo : BANK * (lo + 2)])
+            cols = slice(BANK * j, BANK * (j + 1))
+            bank = banks.tile([P, BANK], F32, tag="bank")
+            nc.tensor.matmul_mx(out=bank[:], lhsT=gated_words[:, tokens].bitcast(FP8X4), lhsT_scale=gated_scales[:, tokens],
+                                rhs=ow_words[:, cols].bitcast(FP8X4), rhs_scale=ow_scales[:, cols], start=True, stop=True)
+            target = result[tile][:, cols].rearrange("p (r x) -> p r x", x=4)
+            nc.vector.tensor_tensor(out=target, in0=bank[:].rearrange("p (x r) -> p r x", x=4), in1=target, op=ADD)
+            nc.sync.dma_start(out=out_v[:, tile, cols], in_=result[tile][:, cols])
 
         copied = []
 
@@ -225,46 +199,37 @@ def tile_aurelianmemorycore_pb_kernel(tc, h, gated_mem, go_w, go_b, out_w, out_b
             catch_up()
             copied.append(unit)
 
-        weights = [gw_unit(u, c) for cs in gw_chunks for u in range(2) for c in cs]
-        projection = [ow_unit(v) for v in range(8)]
-        second, third = gate_in_units(1), gate_in_units(2)
-        early = [(tile, j) for lo in range(0, OUT_BANKS, 2) for tile in GROUPS[0] for j in (lo, lo + 1)]
-
-        for n, unit in enumerate(gate_in_units(0) + weights + projection[:4]):
+        units = [gi_unit(c, pair) for half in range(2) for pair in range(2) for c in (2 * half, 2 * half + 1)]
+        units += [gi_unit(GATE_PASSES - 1, pair) for pair in range(2)]
+        units += [gw_unit(n) for n in range(10)]
+        units += [ow_unit(j, y) for j in range(OUT_BANKS) for y in range(2)]
+        vector_residuals = [(tile, j) for j in range(3) for tile in range(TOKEN_TILES)]
+        for n, unit in enumerate(units):
             prepare(unit)
-            if n == 0:
-                spread_biases()
-                for tiles in GROUPS[1:]:
-                    for j in range(OUT_BANKS):
-                        residual(nc.gpsimd, tiles[0], j)
-            if n >= 2 and n % 2 == 0 and early:
-                tile, j = early.pop(0)
-                residual(nc.vector, tile, j)
+            if n == 3:
+                spread_gate_bias()
+            if n >= 3 and n % 2 == 1 and vector_residuals:
+                tile, j = vector_residuals.pop(0)
+                if j not in bias_banks:
+                    spread_bias(j)
+                residual_vector(tile, j)
+            for t in range(4):
+                if n == 10 + (5 * (t + 1) + 1) // 2 + 1:
+                    gate_of(t)
         catch_up()
-        gate_of(0)
-        product(0, 0)
-        product(0, 1)
+        while vector_residuals:
+            tile, j = vector_residuals.pop(0)
+            residual_vector(tile, j)
+        product(0)
+        product(1)
         quantise_product(0)
+        product(2)
         quantise_product(1)
-        for k in range(4):
-            prepare(projection[4 + k])
-            if k < len(second):
-                prepare(second[k])
-        catch_up()
-        finish_half(0, 0)
-        prepare(third[0])
-        gate_of(1)
-        finish_half(0, 2)
-        prepare(third[1])
-        prepare(third[2])
-        catch_up()
-        product(1, 0)
+        product(3)
         quantise_product(2)
-        finish_half(1, 0)
-        finish_half(1, 2)
-        gate_of(2)
-        product(2, 0)
         quantise_product(3)
-        for tile in (2, 3):
-            finish_half(tile, 0)
-            finish_half(tile, 2)
+        for tile in range(TOKEN_TILES):
+            residual_tensor(tile, 3)
+        for j in range(OUT_BANKS):
+            for tile in range(TOKEN_TILES):
+                finish(tile, j)

@@ -185,7 +185,9 @@ def tile_aurelianmemorycore_pb_kernel(tc, h, gated_mem, go_w, go_b, out_w, out_b
                                 rhs=ow_words[:, cols].bitcast(FP8X4), rhs_scale=ow_scales[:, cols], start=True, stop=True)
             target = result[tile][:, cols].rearrange("p (r x) -> p r x", x=4)
             nc.vector.tensor_tensor(out=target, in0=bank[:].rearrange("p (x r) -> p r x", x=4), in1=target, op=ADD)
-            nc.sync.dma_start(out=out_v[:, tile, cols], in_=result[tile][:, cols])
+            if j % 2 == 1:
+                pair = slice(BANK * (j - 1), BANK * (j + 1))
+                nc.sync.dma_start(out=out_v[:, tile, pair], in_=result[tile][:, pair])
 
         copied = []
 
@@ -230,6 +232,6 @@ def tile_aurelianmemorycore_pb_kernel(tc, h, gated_mem, go_w, go_b, out_w, out_b
         quantise_product(3)
         for tile in range(TOKEN_TILES):
             residual_tensor(tile, 3)
-        for j in range(OUT_BANKS):
-            for tile in range(TOKEN_TILES):
+        for tile in range(TOKEN_TILES):
+            for j in range(OUT_BANKS):
                 finish(tile, j)

@@ -185,7 +185,9 @@ def tile_aurelianmemorycore_pb_kernel(tc, h, gated_mem, go_w, go_b, out_w, out_b
                                 rhs=ow_words[:, cols].bitcast(FP8X4), rhs_scale=ow_scales[:, cols], start=True, stop=True)
             target = result[tile][:, cols].rearrange("p (r x) -> p r x", x=4)
             nc.vector.tensor_tensor(out=target, in0=bank[:].rearrange("p (x r) -> p r x", x=4), in1=target, op=ADD)
-            if j % 2 == 1:
+            if tile == TOKEN_TILES - 1 and j >= 2:
+                nc.sync.dma_start(out=out_v[:, tile, cols], in_=result[tile][:, cols])
+            elif j % 2 == 1:
                 pair = slice(BANK * (j - 1), BANK * (j + 1))
                 nc.sync.dma_start(out=out_v[:, tile, pair], in_=result[tile][:, pair])
 
@@ -231,7 +233,8 @@ def tile_aurelianmemorycore_pb_kernel(tc, h, gated_mem, go_w, go_b, out_w, out_b
         quantise_product(2)
         quantise_product(3)
         for tile in range(TOKEN_TILES):
+            finish(tile, 0)
+            finish(tile, 1)
             residual_tensor(tile, 3)
-        for tile in range(TOKEN_TILES):
-            for j in range(OUT_BANKS):
-                finish(tile, j)
+            finish(tile, 2)
+            finish(tile, 3)

from contextlib import ExitStack

import concourse.mybir as mybir
from concourse.masks import make_identity

F32 = mybir.dt.float32
BF16 = mybir.dt.bfloat16
U32 = mybir.dt.uint32
U8 = mybir.dt.uint8
FP8X4 = mybir.dt.float8_e4m3fn_x4
ADD = mybir.AluOpType.add
MULT = mybir.AluOpType.mult
SIGMOID = mybir.ActivationFunctionType.Sigmoid

P = 128
TOKENS = 512
HIDDEN = 2048
MEMORY = 512
K_GATE = HIDDEN + MEMORY
K_PASS = 4 * P
GATE_PASSES = K_GATE // K_PASS
BANK = 512
TOKEN_TILES = TOKENS // P
OUT_BANKS = HIDDEN // BANK

FLOPS = 2 * TOKENS * K_GATE * MEMORY + 2 * TOKENS * MEMORY * HIDDEN


def tile_aurelianmemorycore_pb_kernel(tc, h, gated_mem, go_w, go_b, out_w, out_b, out):
    nc = tc.nc
    h_v = h.flatten_outer_dims().rearrange("(p i) d -> p i d", i=TOKEN_TILES)
    g_v = gated_mem.flatten_outer_dims().rearrange("(p i) m -> p i m", i=TOKEN_TILES)
    out_v = out.flatten_outer_dims().rearrange("(p i) d -> p i d", i=TOKEN_TILES)
    gw_v = go_w.rearrange("(u p e) k -> p u e k", u=2, e=2)
    ow_v = out_w.rearrange("(j p x) k -> p j x k", j=OUT_BANKS, x=4)

    with ExitStack() as ctx:
        keep = ctx.enter_context(tc.tile_pool(name="keep", bufs=1))
        grouped_pool = ctx.enter_context(tc.tile_pool(name="grouped", bufs=6))
        product_pool = ctx.enter_context(tc.tile_pool(name="product", bufs=4))
        banks = ctx.enter_context(tc.psum_pool(name="banks", bufs=6))
        gate_banks = ctx.enter_context(tc.psum_pool(name="gate_banks", bufs=2))

        bias_row = keep.tile([P, HIDDEN], BF16)
        gate_bias_rows = keep.tile([P, 2 * P], BF16)
        ones = keep.tile([P, P], BF16)
        table_warmer = keep.tile([P, 2], F32)
        identity = keep.tile([P, P], F32)
        identity_bf = keep.tile([P, P], BF16)
        nc.vector.memset(table_warmer[:], 0.0)
        nc.vector.memset(gate_bias_rows[:], 0.0)
        nc.vector.memset(ones[:], 1.0)
        make_identity(nc, identity[:])
        nc.vector.memset(bias_row[:].bitcast(U32), 0)
        nc.vector.tensor_copy(out=identity_bf[:], in_=identity[:])
        nc.scalar.activation(out=table_warmer[:, 1:2], in_=table_warmer[:, 0:1], func=SIGMOID)

        h_sb = [[keep.tile([P, 2, 2 * K_PASS], BF16, name="h_sb%d_%d" % (half, pair)) for pair in range(2)] for half in range(2)]
        g_sb = keep.tile([P, TOKEN_TILES, MEMORY], BF16)
        gw_sb = [keep.tile([P, K_GATE], BF16, name="gw_sb%d" % t) for t in range(4)]
        ow_sb = [keep.tile([P, 4, MEMORY], BF16, name="ow_sb%d" % j) for j in range(OUT_BANKS)]

        def load_h(half, pair):
            nc.sync.dma_start(out=h_sb[half][pair][:], in_=h_v[:, 2 * pair : 2 * pair + 2, 2 * K_PASS * half : 2 * K_PASS * (half + 1)])

        load_h(0, 0)
        load_h(0, 1)
        nc.sync.dma_start(out=bias_row[0:1, :], in_=out_b.rearrange("(o d) -> o d", o=1))
        nc.sync.dma_start(out=gate_bias_rows[0:2, :], in_=go_b.rearrange("(u x) -> u x", u=2))
        load_h(1, 0)
        load_h(1, 1)
        nc.sync.dma_start(out=g_sb[:], in_=g_v)
        for t in range(4):
            nc.sync.dma_start(out=gw_sb[t][:], in_=gw_v[:, t // 2, t % 2, :])
        for j in range(OUT_BANKS):
            nc.sync.dma_start(out=ow_sb[j][:], in_=ow_v[:, j, :, :])

        def h_block(tile, c):
            return h_sb[c // 2][tile // 2][:, tile % 2, K_PASS * (c % 2) : K_PASS * (c % 2 + 1)]

        gi_words = keep.tile([P, GATE_PASSES * TOKENS], U32, align_bytes=64)
        gi_scales = keep.tile([P, GATE_PASSES * TOKENS], U8, align_bytes=64)
        gw_words = keep.tile([P, GATE_PASSES * MEMORY], U32, align_bytes=64)
        gw_scales = keep.tile([P, GATE_PASSES * MEMORY], U8, align_bytes=64)
        ow_words = keep.tile([P, HIDDEN], U32, align_bytes=64)
        ow_scales = keep.tile([P, HIDDEN], U8, align_bytes=64)
        gated_words = keep.tile([P, TOKENS], U32, align_bytes=64)
        gated_scales = keep.tile([P, TOKENS], U8, align_bytes=64)

        memory_t = keep.tile([P, TOKEN_TILES * MEMORY], BF16, align_bytes=64)
        gate = keep.tile([P, 4, TOKENS], F32)
        result = [keep.tile([P, HIDDEN], F32, name="result%d" % i) for i in range(TOKEN_TILES)]
        gate_bias = keep.tile([P, 4], F32)

        def make_unit(blocks, words, scales, grouped=None):
            return {"blocks": blocks, "words": words, "scales": scales, "grouped": grouped}

        def transposes(unit):
            bank = banks.tile([P, 2, 2, P], F32, tag="bank")
            for a, block in enumerate(unit["blocks"]):
                pairs = block.bitcast(F32)
                for u in range(2):
                    nc.tensor.transpose(bank[:, a, u, :], pairs[:, P * u : P * (u + 1)], identity[:])
            unit["bank"] = bank

        def copy_out(unit):
            if unit["grouped"] is None:
                fresh = grouped_pool.tile([P, 2 * K_PASS], BF16, tag="grouped", align_bytes=64)
                unit["grouped"] = fresh[:]
            pairs = unit["grouped"].bitcast(F32)
            nc.scalar.copy(out=pairs.rearrange("p (a r u) -> p a r u", a=2, u=2), in_=unit["bank"][:].rearrange("p a u r -> p a r u"))

        def quantise(unit):
            nc.vector.quantize_mx(out=unit["words"].bitcast(FP8X4), scales=unit["scales"], in_=unit["grouped"])

        def gi_unit(c, pair):
            cols = slice(TOKENS * c + 2 * P * pair, TOKENS * c + 2 * P * (pair + 1))
            if c < GATE_PASSES - 1:
                return make_unit([h_block(2 * pair, c), h_block(2 * pair + 1, c)], gi_words[:, cols], gi_scales[:, cols])
            return make_unit([g_sb[:, 2 * pair, :], g_sb[:, 2 * pair + 1, :]], gi_words[:, cols], gi_scales[:, cols],
                             grouped=memory_t[:, 2 * MEMORY * pair : 2 * MEMORY * (pair + 1)])

        def gw_unit(n):
            cols = slice(2 * P * n, 2 * P * (n + 1))
            blocks = []
            for b in (2 * n, 2 * n + 1):
                t, c = divmod(b, GATE_PASSES)
                blocks.append(gw_sb[t][:, K_PASS * c : K_PASS * (c + 1)])
            return make_unit(blocks, gw_words[:, cols], gw_scales[:, cols])

        def ow_unit(j, y):
            cols = slice(BANK * j + 2 * P * y, BANK * j + 2 * P * (y + 1))
            return make_unit([ow_sb[j][:, 2 * y, :], ow_sb[j][:, 2 * y + 1, :]], ow_words[:, cols], ow_scales[:, cols])

        bias_banks = {}

        def spread_bias(j):
            bank = banks.tile([P, BANK], F32, tag="bank")
            nc.tensor.matmul(out=bank[:], lhsT=ones[:], rhs=bias_row[:, BANK * j : BANK * (j + 1)], start=True, stop=True)
            bias_banks[j] = bank

        def residual_vector(tile, j):
            cols = slice(BANK * j, BANK * (j + 1))
            nc.vector.tensor_tensor(out=result[tile][:, cols], in0=bias_banks[j][:], in1=h_block(tile, j), op=ADD)

        def residual_tensor(tile, j):
            cols = slice(BANK * j, BANK * (j + 1))
            bank = banks.tile([P, BANK], F32, tag="bank")
            nc.tensor.matmul(out=bank[:], lhsT=identity_bf[:], rhs=h_block(tile, j), start=True, stop=False)
            nc.tensor.matmul(out=bank[:], lhsT=ones[:], rhs=bias_row[:, cols], start=False, stop=True)
            nc.scalar.copy(out=result[tile][:, cols], in_=bank[:])

        def spread_gate_bias():
            pairs = banks.tile([P, P], F32, tag="bank")
            nc.tensor.transpose(pairs[:], gate_bias_rows[:].bitcast(F32), identity[:])
            nc.vector.tensor_copy(out=gate_bias[:], in_=pairs[:, 0:2].bitcast(BF16))

        def gate_of(t):
            sums = gate_banks.tile([P, TOKENS], F32, tag="sums", name="sums")
            for c in range(GATE_PASSES):
                w = slice(P * (GATE_PASSES * t + c), P * (GATE_PASSES * t + c + 1))
                x = slice(TOKENS * c, TOKENS * (c + 1))
                nc.tensor.matmul_mx(out=sums[:], lhsT=gw_words[:, w].bitcast(FP8X4), lhsT_scale=gw_scales[:, w],
                                    rhs=gi_words[:, x].bitcast(FP8X4), rhs_scale=gi_scales[:, x],
                                    start=(c == 0), stop=(c == GATE_PASSES - 1))
            nc.scalar.activation(out=gate[:, t, :], in_=sums[:], func=SIGMOID, bias=gate_bias[:, t : t + 1], scale=1.0)

        gated = {}

        def product(tile):
            gated[tile] = product_pool.tile([P, K_PASS], BF16, tag="gated", name="gated", align_bytes=64)
            nc.vector.tensor_tensor(out=gated[tile][:].rearrange("p (r t) -> p r t", t=4),
                                    in0=gate[:, :, P * tile : P * (tile + 1)].rearrange("p t r -> p r t"),
                                    in1=memory_t[:, MEMORY * tile : MEMORY * (tile + 1)].rearrange("p (r t) -> p r t", t=4), op=MULT)

        def quantise_product(tile):
            cols = slice(P * tile, P * (tile + 1))
            nc.vector.quantize_mx(out=gated_words[:, cols].bitcast(FP8X4), scales=gated_scales[:, cols], in_=gated[tile][:])

        def finish(tile, j):
            tokens = slice(P * tile, P * (tile + 1))
            cols = slice(BANK * j, BANK * (j + 1))
            bank = banks.tile([P, BANK], F32, tag="bank")
            nc.tensor.matmul_mx(out=bank[:], lhsT=gated_words[:, tokens].bitcast(FP8X4), lhsT_scale=gated_scales[:, tokens],
                                rhs=ow_words[:, cols].bitcast(FP8X4), rhs_scale=ow_scales[:, cols], start=True, stop=True)
            target = result[tile][:, cols].rearrange("p (r x) -> p r x", x=4)
            nc.vector.tensor_tensor(out=target, in0=bank[:].rearrange("p (x r) -> p r x", x=4), in1=target, op=ADD)
            if tile == TOKEN_TILES - 1 and j >= 2:
                nc.sync.dma_start(out=out_v[:, tile, cols], in_=result[tile][:, cols])
            elif j % 2 == 1:
                pair = slice(BANK * (j - 1), BANK * (j + 1))
                nc.sync.dma_start(out=out_v[:, tile, pair], in_=result[tile][:, pair])

        copied = []

        def catch_up():
            if copied:
                quantise(copied.pop())

        def prepare(unit):
            transposes(unit)
            copy_out(unit)
            catch_up()
            copied.append(unit)

        units = [gi_unit(c, pair) for half in range(2) for pair in range(2) for c in (2 * half, 2 * half + 1)]
        units += [gi_unit(GATE_PASSES - 1, pair) for pair in range(2)]
        units += [gw_unit(n) for n in range(10)]
        units += [ow_unit(j, y) for j in range(OUT_BANKS) for y in range(2)]
        vector_residuals = [(tile, j) for j in range(3) for tile in range(TOKEN_TILES)]
        for n, unit in enumerate(units):
            prepare(unit)
            if n == 3:
                spread_gate_bias()
            if n >= 3 and n % 2 == 1 and vector_residuals:
                tile, j = vector_residuals.pop(0)
                if j not in bias_banks:
                    spread_bias(j)
                residual_vector(tile, j)
            for t in range(4):
                if n == 10 + (5 * (t + 1) + 1) // 2 + 1:
                    gate_of(t)
        catch_up()
        while vector_residuals:
            tile, j = vector_residuals.pop(0)
            residual_vector(tile, j)
        product(0)
        product(1)
        quantise_product(0)
        product(2)
        quantise_product(1)
        product(3)
        quantise_product(2)
        quantise_product(3)
        for tile in range(TOKEN_TILES):
            finish(tile, 0)
            finish(tile, 1)
            residual_tensor(tile, 3)
            finish(tile, 2)
            finish(tile, 3)
